import numpy as np
import ml_dtypes


def mxq(x, axis, fmt="e4m3"):
    dtype, down = {"e4m3": (ml_dtypes.float8_e4m3fn, 7), "e5m2": (ml_dtypes.float8_e5m2, 14)}[fmt]
    v = np.moveaxis(np.asarray(x, np.float32).astype(ml_dtypes.bfloat16).astype(np.float64), axis, -1)
    blocks = v.reshape(v.shape[:-1] + (-1, 32))
    amax = np.abs(blocks).max(-1, keepdims=True)
    byte = np.maximum(np.where(amax > 0, np.frexp(amax)[1] - 1 + 127, 0) - down, 1)
    scale = np.exp2(byte - 127.0)
    codes = (blocks / scale).astype(np.float32).astype(dtype).astype(np.float64)
    return np.moveaxis((codes * scale).reshape(v.shape), -1, axis)


WIDE = False


def mx_kscale(k):
    if not WIDE:
        return np.ones(k)
    levels = np.array([10, -10, 5, -5, 0])
    a = np.random.permutation(np.resize(levels, k // 512 * 4)).reshape(k // 512, 4)
    idx = np.arange(k)
    return np.exp2(a[idx // 512, idx % 128 // 32])


BF16 = ml_dtypes.bfloat16


def bf(x):
    return np.asarray(x, np.float32).astype(BF16)


def f64(x):
    return np.asarray(x).astype(np.float64)


B, H, O, I, K = 4096, 1024, 16, 16, 1024


def silu(v):
    return v / (1.0 + np.exp(-v))


def setup_inputs():
    s = mx_kscale(H)
    return {
        "hk": bf(silu(np.random.standard_normal((B, H))) * s),
        "kw2": bf(np.random.standard_normal((H, K)) * 1.5 / np.sqrt(H) / s[:, None]),
        "kb2": bf(np.random.standard_normal(K) * 0.3),
        "bases": bf(np.random.standard_normal((K, O, I)) * 1.5 / np.sqrt(K)),
        "base": bf(np.random.standard_normal((O, I)) * 0.7),
        "row": bf(1.0 + 0.1 * np.tanh(np.random.standard_normal((B, O)))),
        "col": bf(1.0 + 0.1 * np.tanh(np.random.standard_normal((B, I)))),
    }


def reference(hk, kw2, kb2, bases, base, row, col):
    coeff = np.tanh((mxq(f64(hk), 1, "e4m3") @ mxq(f64(kw2), 0, "e4m3")) + f64(kb2))
    delta = (mxq(coeff, 1, "e4m3") @ mxq(f64(bases).reshape(K, O * I), 0, "e4m3")).reshape(B, O, I)
    weight = (f64(base)[None] + delta) * f64(row)[:, :, None] * f64(col)[:, None, :]
    return weight, coeff

@@ -1,0 +1,329 @@
+from contextlib import ExitStack
+
+import concourse.mybir as mybir
+from concourse.masks import make_identity
+
+F32 = mybir.dt.float32
+BF16 = mybir.dt.bfloat16
+U32 = mybir.dt.uint32
+U8 = mybir.dt.uint8
+FP8X4 = mybir.dt.float8_e4m3fn_x4
+TANH = mybir.ActivationFunctionType.Tanh
+ADD = mybir.AluOpType.add
+MULT = mybir.AluOpType.mult
+
+P = 128
+PACK = 4
+K_PASS = P * PACK
+BANK = 512
+
+B = 4096
+H = 1024
+K = 1024
+O = 16
+I = 16
+OI = O * I
+H_PASSES = H // K_PASS
+K_PASSES = K // K_PASS
+ROWS_PER_PARTITION = B // P
+CHUNK_TILES = 4
+CHUNK = CHUNK_TILES * P
+CHUNKS = B // CHUNK
+STEPS = CHUNKS * K_PASSES
+HK_UNITS = CHUNKS * H_PASSES
+HK_AHEAD = 3
+
+FLOPS = 2 * B * H * K + 2 * B * K * OI
+
+
+def tile_structuredternaryfactorgenerator_pa_t_kernel(
+    tc, hk, kw2, kb2, bases, base, row, col, out_0, out_1
+):
+    nc = tc.nc
+
+    hk_rows = hk.rearrange("(p j) h -> p j h", j=ROWS_PER_PARTITION)
+    coeff_rows = out_1.rearrange("(p j) k -> p j k", j=ROWS_PER_PARTITION)
+    weight_rows = out_0.rearrange("(p j) o i -> p j (o i)", j=ROWS_PER_PARTITION)
+
+    with ExitStack() as stack:
+        const = stack.enter_context(tc.tile_pool(name="const", bufs=1))
+        setup = stack.enter_context(tc.tile_pool(name="setup", bufs=1))
+        stream = stack.enter_context(tc.tile_pool(name="stream", bufs=2))
+        psum_hk = stack.enter_context(tc.psum_pool(name="psum_hk", bufs=2))
+        psum_s1 = stack.enter_context(tc.psum_pool(name="psum_s1", bufs=3))
+        psum_co = stack.enter_context(tc.psum_pool(name="psum_co", bufs=2))
+        psum_s2 = stack.enter_context(tc.psum_pool(name="psum_s2", bufs=1))
+        stack.enter_context(tc.manual_schedule())
+
+        hk_tiles = {}
+        hk_grouped_tiles = {}
+        hk_quantised = {}
+        coeff_t_tiles = {}
+        coeff_grouped_tiles = {}
+        coeff_quantised = {}
+        coeff_sb_tiles = {}
+        gains_tiles = {}
+        weight_sb_tiles = {}
+
+        def load_hk(c):
+            hk_sb = stream.tile([P, CHUNK_TILES * H], BF16, bufs=3)
+            nc.sync.dma_start(
+                out=hk_sb[:].rearrange("p (j h) -> p j h", j=CHUNK_TILES),
+                in_=hk_rows[:, c * CHUNK_TILES : (c + 1) * CHUNK_TILES, :],
+            )
+            hk_tiles[c] = hk_sb
+
+        kw_raw = setup.tile([P, K_PASSES, H_PASSES * PACK, K_PASS], BF16)
+        kw_view = kw2.rearrange("(a w e) k -> e w a k", w=P, e=2)
+
+        def load_kw(G):
+            for e in range(2):
+                nc.sync.dma_start(
+                    out=kw_raw[:, G, :, :].rearrange("p (a e) k -> p a e k", e=2)[:, :, e, :],
+                    in_=kw_view[e][:, :, G * K_PASS : (G + 1) * K_PASS],
+                )
+
+        load_kw(0)
+        load_hk(0)
+        load_hk(1)
+        load_kw(1)
+        load_hk(2)
+
+        kb_rows = setup.tile([P, P], BF16)
+        nc.vector.memset(kb_rows[:], 0.0)
+        nc.scalar.dma_start(out=kb_rows[0 : K // P, :], in_=kb2.rearrange("(m p) -> m p", p=P))
+        bases_raw = setup.tile([P, K_PASSES * PACK, OI], BF16)
+        nc.scalar.dma_start(out=bases_raw[:], in_=bases.rearrange("(a p) o i -> p a (o i)", p=P))
+        base_row = setup.tile([P, OI], BF16)
+        nc.vector.memset(base_row[:], 0.0)
+        nc.scalar.dma_start(out=base_row[0:1, :], in_=base.rearrange("(a o) i -> a (o i)", a=1))
+        row_sb = const.tile([P, ROWS_PER_PARTITION, O], BF16)
+        nc.scalar.dma_start(
+            out=row_sb[:], in_=row.rearrange("(p j) o -> p j o", j=ROWS_PER_PARTITION)
+        )
+        col_sb = const.tile([P, ROWS_PER_PARTITION, I], BF16)
+        nc.scalar.dma_start(
+            out=col_sb[:], in_=col.rearrange("(p j) i -> p j i", j=ROWS_PER_PARTITION)
+        )
+
+        ident = const.tile([P, P], F32)
+        make_identity(nc, ident[:])
+        ones = const.tile([P, P], BF16)
+        nc.vector.memset(ones[:], 1.0)
+
+        kb_rows_f32 = setup.tile([P, P], F32)
+        nc.vector.tensor_copy(out=kb_rows_f32[:], in_=kb_rows[:])
+        kb_bank = psum_co.tile([P, BANK], F32, name="co_bank")
+        nc.tensor.transpose(kb_bank[:, 0:P], kb_rows_f32[:], ident[:])
+        kb = const.tile([P, K // P], F32)
+        nc.vector.tensor_copy(out=kb[:], in_=kb_bank[:, 0 : K // P])
+
+        kw_codes = const.tile([P, K_PASSES, H_PASSES, K_PASS], U32, align_bytes=64)
+        kw_scales = const.tile([P, K_PASSES, H_PASSES, K_PASS], U8, align_bytes=64)
+        bases_codes = const.tile([P, K_PASSES, OI], U32, align_bytes=64)
+        bases_scales = const.tile([P, K_PASSES, OI], U8, align_bytes=64)
+        base_all = const.tile([P, OI], F32)
+
+        def quantise_kw(G):
+            kw_grouped = setup.tile([P, H_PASSES, K_PASS, PACK], BF16, align_bytes=64, bufs=2)
+            for g in range(H_PASSES):
+                nc.vector.tensor_copy(
+                    out=kw_grouped[:, g, :, :].rearrange("p (c i) t -> p c t i", i=4),
+                    in_=kw_raw[:, G, g * PACK : (g + 1) * PACK, :].rearrange(
+                        "p t (c i) -> p c t i", i=4
+                    ),
+                )
+            nc.vector.quantize_mx(
+                out=kw_codes[:, G, :, :].rearrange("p g k -> p (g k)").bitcast(FP8X4),
+                scales=kw_scales[:, G, :, :].rearrange("p g k -> p (g k)"),
+                in_=kw_grouped[:].rearrange("p g k t -> p (g k t)"),
+            )
+
+        def prepare_stage_2():
+            bases_grouped = setup.tile([P, K_PASSES, OI, PACK], BF16, align_bytes=64)
+            nc.vector.tensor_copy(
+                out=bases_grouped[:], in_=bases_raw[:].rearrange("p (G t) n -> p G n t", t=PACK)
+            )
+            base_bank = psum_co.tile([P, BANK], F32, name="co_bank")
+            nc.tensor.matmul(
+                base_bank[:, 0:OI], lhsT=ones[:], rhs=base_row[:], start=True, stop=True
+            )
+            nc.vector.tensor_copy(out=base_all[:], in_=base_bank[:, 0:OI])
+            nc.vector.quantize_mx(
+                out=bases_codes[:].rearrange("p G n -> p (G n)").bitcast(FP8X4),
+                scales=bases_scales[:].rearrange("p G n -> p (G n)"),
+                in_=bases_grouped[:].rearrange("p G n t -> p (G n t)"),
+            )
+
+        def transpose_hk(unit, copy_out):
+            c, g = divmod(unit, H_PASSES)
+            hk_words = hk_tiles[c][:].bitcast(F32)
+            words_per_row = H // 2
+            hk_grouped = stream.tile([P, CHUNK * PACK], BF16, align_bytes=64, bufs=HK_AHEAD)
+            grouped_words = hk_grouped[:].bitcast(F32).rearrange("p (b u) -> p b u", u=2)
+            for pair in range(CHUNK_TILES // 2):
+                hk_bank = psum_hk.tile([P, BANK], F32)
+                for u in range(2):
+                    for jj in range(2):
+                        first = (2 * pair + jj) * words_per_row + (2 * g + u) * P
+                        nc.tensor.transpose(
+                            hk_bank[:, (2 * u + jj) * P : (2 * u + jj + 1) * P],
+                            hk_words[:, first : first + P],
+                            ident[:],
+                        )
+                copy_out(
+                    out=grouped_words[:, 2 * pair * P : (2 * pair + 2) * P, :],
+                    in_=hk_bank[:].rearrange("p (u b) -> p b u", u=2),
+                )
+            hk_grouped_tiles[unit] = hk_grouped
+
+        def quantise_hk(unit):
+            hk_codes = stream.tile([P, CHUNK], U32, align_bytes=64, bufs=4)
+            hk_scales = stream.tile([P, CHUNK], U8, align_bytes=64, bufs=4)
+            nc.vector.quantize_mx(
+                out=hk_codes[:].bitcast(FP8X4), scales=hk_scales[:], in_=hk_grouped_tiles[unit][:]
+            )
+            hk_quantised[unit] = (hk_codes, hk_scales)
+
+        def stage_1(s):
+            c, G = divmod(s, K_PASSES)
+            coeff_t = stream.tile([P, PACK, CHUNK], F32, bufs=3)
+            for t in range(PACK):
+                s1_bank = psum_s1.tile([P, BANK], F32)
+                for g in range(H_PASSES):
+                    hk_codes, hk_scales = hk_quantised[c * H_PASSES + g]
+                    nc.tensor.matmul_mx(
+                        out=s1_bank[:],
+                        lhsT=kw_codes[:, G, g, t * P : (t + 1) * P].bitcast(FP8X4),
+                        lhsT_scale=kw_scales[:, G, g, t * P : (t + 1) * P],
+                        rhs=hk_codes[:].bitcast(FP8X4),
+                        rhs_scale=hk_scales[:],
+                        start=(g == 0),
+                        stop=(g == H_PASSES - 1),
+                    )
+                m = G * PACK + t
+                nc.scalar.activation(
+                    out=coeff_t[:, t, :], in_=s1_bank[:], func=TANH, bias=kb[:, m : m + 1]
+                )
+            coeff_t_tiles[s] = coeff_t
+
+        def regroup_coeff(s):
+            coeff_grouped = stream.tile([P, CHUNK, PACK], BF16, align_bytes=64)
+            nc.vector.tensor_copy(
+                out=coeff_grouped[:], in_=coeff_t_tiles[s][:].rearrange("p t b -> p b t")
+            )
+            coeff_grouped_tiles[s] = coeff_grouped
+
+        def quantise_coeff(s):
+            coeff_codes = stream.tile([P, CHUNK], U32, align_bytes=64, bufs=4)
+            coeff_scales = stream.tile([P, CHUNK], U8, align_bytes=64, bufs=4)
+            nc.vector.quantize_mx(
+                out=coeff_codes[:].bitcast(FP8X4),
+                scales=coeff_scales[:],
+                in_=coeff_grouped_tiles[s][:].rearrange("p b t -> p (b t)"),
+            )
+            coeff_quantised[s] = (coeff_codes, coeff_scales)
+
+        def transpose_coeff(s, pair):
+            c, G = divmod(s, K_PASSES)
+            if G == 0 and pair == 0:
+                coeff_sb_tiles[c] = stream.tile([P, CHUNK_TILES, K], F32, name="coeff_sb", bufs=3)
+            coeff_sb = coeff_sb_tiles[c]
+            for j in range(2 * pair, 2 * pair + 2):
+                co_bank = psum_co.tile([P, BANK], F32)
+                for t in range(PACK):
+                    nc.tensor.transpose(
+                        co_bank[:, t * P : (t + 1) * P],
+                        coeff_t_tiles[s][:, t, j * P : (j + 1) * P],
+                        ident[:],
+                    )
+                nc.scalar.copy(out=coeff_sb[:, j, G * BANK : (G + 1) * BANK], in_=co_bank[:])
+            if G == K_PASSES - 1:
+                first = c * CHUNK_TILES + 2 * pair
+                nc.sync.dma_start(
+                    out=coeff_rows[:, first : first + 2, :],
+                    in_=coeff_sb[:, 2 * pair : 2 * pair + 2, :],
+                )
+
+        def compute_gains(c):
+            rows = slice(c * CHUNK_TILES, (c + 1) * CHUNK_TILES)
+            gains = stream.tile([P, CHUNK_TILES, O, I], F32)
+            nc.gpsimd.tensor_tensor(
+                out=gains[:],
+                in0=row_sb[:, rows, :].unsqueeze(3).to_broadcast([P, CHUNK_TILES, O, I]),
+                in1=col_sb[:, rows, :].unsqueeze(2).to_broadcast([P, CHUNK_TILES, O, I]),
+                op=MULT,
+            )
+            gains_tiles[c] = gains
+
+        def stage_2(v):
+            c, pair = divmod(v, 2)
+            if pair == 0:
+                weight_sb_tiles[c] = stream.tile([P, CHUNK_TILES, OI], F32, name="weight_sb")
+            weight_sb = weight_sb_tiles[c]
+            s2_bank = psum_s2.tile([P, 2, OI], F32)
+            for jj in range(2):
+                j = 2 * pair + jj
+                for G in range(K_PASSES):
+                    coeff_codes, coeff_scales = coeff_quantised[c * K_PASSES + G]
+                    nc.tensor.matmul_mx(
+                        out=s2_bank[:, jj, :],
+                        lhsT=coeff_codes[:, j * P : (j + 1) * P].bitcast(FP8X4),
+                        lhsT_scale=coeff_scales[:, j * P : (j + 1) * P],
+                        rhs=bases_codes[:, G, :].bitcast(FP8X4),
+                        rhs_scale=bases_scales[:, G, :],
+                        start=(G == 0),
+                        stop=(G == K_PASSES - 1),
+                    )
+            summed = stream.tile([P, 2, OI], F32)
+            nc.vector.tensor_tensor(
+                out=summed[:],
+                in0=s2_bank[:],
+                in1=base_all[:].unsqueeze(1).to_broadcast([P, 2, OI]),
+                op=ADD,
+            )
+            js = slice(2 * pair, 2 * pair + 2)
+            nc.gpsimd.tensor_tensor(
+                out=weight_sb[:, js, :],
+                in0=summed[:],
+                in1=gains_tiles[c][:].rearrange("p j o i -> p j (o i)")[:, js, :],
+                op=MULT,
+            )
+            if pair == 1:
+                nc.sync.dma_start(
+                    out=weight_rows[:, c * CHUNK_TILES : (c + 1) * CHUNK_TILES, :], in_=weight_sb[:]
+                )
+
+        def step(s):
+            has_previous = 1 <= s <= STEPS
+            if s % 2 == 0 and s // 2 + 3 < CHUNKS:
+                load_hk(s // 2 + 3)
+            if s % 2 == 1 and s // 2 < CHUNKS:
+                compute_gains(s // 2)
+            if has_previous:
+                regroup_coeff(s - 1)
+            if s + HK_AHEAD - 1 < HK_UNITS:
+                quantise_hk(s + HK_AHEAD - 1)
+            if has_previous:
+                quantise_coeff(s - 1)
+            if has_previous:
+                transpose_coeff(s - 1, 0)
+            if s + HK_AHEAD < HK_UNITS:
+                transpose_hk(s + HK_AHEAD, nc.vector.tensor_copy)
+            if has_previous:
+                transpose_coeff(s - 1, 1)
+            if s < STEPS:
+                stage_1(s)
+            if 0 <= s - 2 < STEPS:
+                stage_2(s - 2)
+
+        quantise_kw(0)
+        for unit in range(HK_AHEAD):
+            transpose_hk(unit, nc.scalar.copy)
+        for unit in range(HK_AHEAD - 1):
+            quantise_hk(unit)
+        quantise_kw(1)
+        step(0)
+        prepare_stage_2()
+        for s in range(1, STEPS + 2):
+            step(s)

@@ -64,6 +64,7 @@ def tile_structuredternaryfactorgenerator_pa_t_kernel(
         coeff_sb_tiles = {}
         gains_tiles = {}
         weight_sb_tiles = {}
+        s2_banks = {}
 
         def load_hk(c):
             hk_sb = stream.tile([P, CHUNK_TILES * H], BF16, bufs=3)
@@ -155,27 +156,28 @@ def tile_structuredternaryfactorgenerator_pa_t_kernel(
                 in_=bases_grouped[:].rearrange("p G n t -> p (G n t)"),
             )
 
-        def transpose_hk(unit, copy_out):
+        def transpose_hk(unit, pair, copy_out):
             c, g = divmod(unit, H_PASSES)
             hk_words = hk_tiles[c][:].bitcast(F32)
             words_per_row = H // 2
-            hk_grouped = stream.tile([P, CHUNK * PACK], BF16, align_bytes=64, bufs=HK_AHEAD)
-            grouped_words = hk_grouped[:].bitcast(F32).rearrange("p (b u) -> p b u", u=2)
-            for pair in range(CHUNK_TILES // 2):
-                hk_bank = psum_hk.tile([P, BANK], F32)
-                for u in range(2):
-                    for jj in range(2):
-                        first = (2 * pair + jj) * words_per_row + (2 * g + u) * P
-                        nc.tensor.transpose(
-                            hk_bank[:, (2 * u + jj) * P : (2 * u + jj + 1) * P],
-                            hk_words[:, first : first + P],
-                            ident[:],
-                        )
-                copy_out(
-                    out=grouped_words[:, 2 * pair * P : (2 * pair + 2) * P, :],
-                    in_=hk_bank[:].rearrange("p (u b) -> p b u", u=2),
+            if pair == 0:
+                hk_grouped_tiles[unit] = stream.tile(
+                    [P, CHUNK * PACK], BF16, name="hk_grouped", align_bytes=64, bufs=HK_AHEAD
                 )
-            hk_grouped_tiles[unit] = hk_grouped
+            grouped_words = hk_grouped_tiles[unit][:].bitcast(F32).rearrange("p (b u) -> p b u", u=2)
+            hk_bank = psum_hk.tile([P, BANK], F32)
+            for u in range(2):
+                for jj in range(2):
+                    first = (2 * pair + jj) * words_per_row + (2 * g + u) * P
+                    nc.tensor.transpose(
+                        hk_bank[:, (2 * u + jj) * P : (2 * u + jj + 1) * P],
+                        hk_words[:, first : first + P],
+                        ident[:],
+                    )
+            copy_out(
+                out=grouped_words[:, 2 * pair * P : (2 * pair + 2) * P, :],
+                in_=hk_bank[:].rearrange("p (u b) -> p b u", u=2),
+            )
 
         def quantise_hk(unit):
             hk_codes = stream.tile([P, CHUNK], U32, align_bytes=64, bufs=4)
@@ -185,10 +187,12 @@ def tile_structuredternaryfactorgenerator_pa_t_kernel(
             )
             hk_quantised[unit] = (hk_codes, hk_scales)
 
-        def stage_1(s):
+        def stage_1(s, half):
             c, G = divmod(s, K_PASSES)
-            coeff_t = stream.tile([P, PACK, CHUNK], F32, bufs=3)
-            for t in range(PACK):
+            if half == 0:
+                coeff_t_tiles[s] = stream.tile([P, PACK, CHUNK], F32, name="coeff_t", bufs=3)
+            coeff_t = coeff_t_tiles[s]
+            for t in range(2 * half, 2 * half + 2):
                 s1_bank = psum_s1.tile([P, BANK], F32)
                 for g in range(H_PASSES):
                     hk_codes, hk_scales = hk_quantised[c * H_PASSES + g]
@@ -205,7 +209,6 @@ def tile_structuredternaryfactorgenerator_pa_t_kernel(
                 nc.scalar.activation(
                     out=coeff_t[:, t, :], in_=s1_bank[:], func=TANH, bias=kb[:, m : m + 1]
                 )
-            coeff_t_tiles[s] = coeff_t
 
         def regroup_coeff(s):
             coeff_grouped = stream.tile([P, CHUNK, PACK], BF16, align_bytes=64)
@@ -256,25 +259,28 @@ def tile_structuredternaryfactorgenerator_pa_t_kernel(
             )
             gains_tiles[c] = gains
 
-        def stage_2(v):
+        def stage_2(v, jj):
             c, pair = divmod(v, 2)
+            if jj == 0:
+                s2_banks[v] = psum_s2.tile([P, 2, OI], F32, name="s2_bank")
+            s2_bank = s2_banks[v]
+            j = 2 * pair + jj
+            for G in range(K_PASSES):
+                coeff_codes, coeff_scales = coeff_quantised[c * K_PASSES + G]
+                nc.tensor.matmul_mx(
+                    out=s2_bank[:, jj, :],
+                    lhsT=coeff_codes[:, j * P : (j + 1) * P].bitcast(FP8X4),
+                    lhsT_scale=coeff_scales[:, j * P : (j + 1) * P],
+                    rhs=bases_codes[:, G, :].bitcast(FP8X4),
+                    rhs_scale=bases_scales[:, G, :],
+                    start=(G == 0),
+                    stop=(G == K_PASSES - 1),
+                )
+            if jj == 0:
+                return
             if pair == 0:
                 weight_sb_tiles[c] = stream.tile([P, CHUNK_TILES, OI], F32, name="weight_sb")
             weight_sb = weight_sb_tiles[c]
-            s2_bank = psum_s2.tile([P, 2, OI], F32)
-            for jj in range(2):
-                j = 2 * pair + jj
-                for G in range(K_PASSES):
-                    coeff_codes, coeff_scales = coeff_quantised[c * K_PASSES + G]
-                    nc.tensor.matmul_mx(
-                        out=s2_bank[:, jj, :],
-                        lhsT=coeff_codes[:, j * P : (j + 1) * P].bitcast(FP8X4),
-                        lhsT_scale=coeff_scales[:, j * P : (j + 1) * P],
-                        rhs=bases_codes[:, G, :].bitcast(FP8X4),
-                        rhs_scale=bases_scales[:, G, :],
-                        start=(G == 0),
-                        stop=(G == K_PASSES - 1),
-                    )
             summed = stream.tile([P, 2, OI], F32)
             nc.vector.tensor_tensor(
                 out=summed[:],
@@ -306,20 +312,20 @@ def tile_structuredternaryfactorgenerator_pa_t_kernel(
                 quantise_hk(s + HK_AHEAD - 1)
             if has_previous:
                 quantise_coeff(s - 1)
-            if has_previous:
-                transpose_coeff(s - 1, 0)
-            if s + HK_AHEAD < HK_UNITS:
-                transpose_hk(s + HK_AHEAD, nc.vector.tensor_copy)
-            if has_previous:
-                transpose_coeff(s - 1, 1)
-            if s < STEPS:
-                stage_1(s)
-            if 0 <= s - 2 < STEPS:
-                stage_2(s - 2)
+            for half in range(2):
+                if has_previous:
+                    transpose_coeff(s - 1, half)
+                if s + HK_AHEAD < HK_UNITS:
+                    transpose_hk(s + HK_AHEAD, half, nc.vector.tensor_copy)
+                if s < STEPS:
+                    stage_1(s, half)
+                if 0 <= s - 2 < STEPS:
+                    stage_2(s - 2, half)
 
         quantise_kw(0)
         for unit in range(HK_AHEAD):
-            transpose_hk(unit, nc.scalar.copy)
+            for pair in range(2):
+                transpose_hk(unit, pair, nc.scalar.copy)
         for unit in range(HK_AHEAD - 1):
             quantise_hk(unit)
         quantise_kw(1)

@@ -32,6 +32,8 @@ CHUNKS = B // CHUNK
 STEPS = CHUNKS * K_PASSES
 HK_UNITS = CHUNKS * H_PASSES
 HK_AHEAD = 3
+COEFF_OUT_LAG = 2
+STAGE_2_LAG = 3
 
 FLOPS = 2 * B * H * K + 2 * B * K * OI
 
@@ -64,7 +66,7 @@ def tile_structuredternaryfactorgenerator_pa_t_kernel(
         coeff_sb_tiles = {}
         gains_tiles = {}
         weight_sb_tiles = {}
-        s2_banks = {}
+        summed_tiles = {}
 
         def load_hk(c):
             hk_sb = stream.tile([P, CHUNK_TILES * H], BF16, bufs=3)
@@ -125,10 +127,10 @@ def tile_structuredternaryfactorgenerator_pa_t_kernel(
         bases_scales = const.tile([P, K_PASSES, OI], U8, align_bytes=64)
         base_all = const.tile([P, OI], F32)
 
-        def quantise_kw(G):
+        def quantise_kw(G, copy_of_pass):
             kw_grouped = setup.tile([P, H_PASSES, K_PASS, PACK], BF16, align_bytes=64, bufs=2)
             for g in range(H_PASSES):
-                nc.vector.tensor_copy(
+                copy_of_pass[g](
                     out=kw_grouped[:, g, :, :].rearrange("p (c i) t -> p c t i", i=4),
                     in_=kw_raw[:, G, g * PACK : (g + 1) * PACK, :].rearrange(
                         "p t (c i) -> p c t i", i=4
@@ -142,7 +144,7 @@ def tile_structuredternaryfactorgenerator_pa_t_kernel(
 
         def prepare_stage_2():
             bases_grouped = setup.tile([P, K_PASSES, OI, PACK], BF16, align_bytes=64)
-            nc.vector.tensor_copy(
+            nc.scalar.copy(
                 out=bases_grouped[:], in_=bases_raw[:].rearrange("p (G t) n -> p G n t", t=PACK)
             )
             base_bank = psum_co.tile([P, BANK], F32, name="co_bank")
@@ -156,28 +158,27 @@ def tile_structuredternaryfactorgenerator_pa_t_kernel(
                 in_=bases_grouped[:].rearrange("p G n t -> p (G n t)"),
             )
 
-        def transpose_hk(unit, pair, copy_out):
+        def transpose_hk(unit, copy_out):
             c, g = divmod(unit, H_PASSES)
             hk_words = hk_tiles[c][:].bitcast(F32)
             words_per_row = H // 2
-            if pair == 0:
-                hk_grouped_tiles[unit] = stream.tile(
-                    [P, CHUNK * PACK], BF16, name="hk_grouped", align_bytes=64, bufs=HK_AHEAD
+            hk_grouped = stream.tile([P, CHUNK * PACK], BF16, align_bytes=64, bufs=HK_AHEAD)
+            grouped_words = hk_grouped[:].bitcast(F32).rearrange("p (b u) -> p b u", u=2)
+            for pair in range(CHUNK_TILES // 2):
+                hk_bank = psum_hk.tile([P, BANK], F32)
+                for u in range(2):
+                    for jj in range(2):
+                        first = (2 * pair + jj) * words_per_row + (2 * g + u) * P
+                        nc.tensor.transpose(
+                            hk_bank[:, (2 * u + jj) * P : (2 * u + jj + 1) * P],
+                            hk_words[:, first : first + P],
+                            ident[:],
+                        )
+                copy_out(
+                    out=grouped_words[:, 2 * pair * P : (2 * pair + 2) * P, :],
+                    in_=hk_bank[:].rearrange("p (u b) -> p b u", u=2),
                 )
-            grouped_words = hk_grouped_tiles[unit][:].bitcast(F32).rearrange("p (b u) -> p b u", u=2)
-            hk_bank = psum_hk.tile([P, BANK], F32)
-            for u in range(2):
-                for jj in range(2):
-                    first = (2 * pair + jj) * words_per_row + (2 * g + u) * P
-                    nc.tensor.transpose(
-                        hk_bank[:, (2 * u + jj) * P : (2 * u + jj + 1) * P],
-                        hk_words[:, first : first + P],
-                        ident[:],
-                    )
-            copy_out(
-                out=grouped_words[:, 2 * pair * P : (2 * pair + 2) * P, :],
-                in_=hk_bank[:].rearrange("p (u b) -> p b u", u=2),
-            )
+            hk_grouped_tiles[unit] = hk_grouped
 
         def quantise_hk(unit):
             hk_codes = stream.tile([P, CHUNK], U32, align_bytes=64, bufs=4)
@@ -187,12 +188,10 @@ def tile_structuredternaryfactorgenerator_pa_t_kernel(
             )
             hk_quantised[unit] = (hk_codes, hk_scales)
 
-        def stage_1(s, half):
+        def stage_1(s):
             c, G = divmod(s, K_PASSES)
-            if half == 0:
-                coeff_t_tiles[s] = stream.tile([P, PACK, CHUNK], F32, name="coeff_t", bufs=3)
-            coeff_t = coeff_t_tiles[s]
-            for t in range(2 * half, 2 * half + 2):
+            coeff_t = stream.tile([P, PACK, CHUNK], F32, bufs=3)
+            for t in range(PACK):
                 s1_bank = psum_s1.tile([P, BANK], F32)
                 for g in range(H_PASSES):
                     hk_codes, hk_scales = hk_quantised[c * H_PASSES + g]
@@ -209,6 +208,7 @@ def tile_structuredternaryfactorgenerator_pa_t_kernel(
                 nc.scalar.activation(
                     out=coeff_t[:, t, :], in_=s1_bank[:], func=TANH, bias=kb[:, m : m + 1]
                 )
+            coeff_t_tiles[s] = coeff_t
 
         def regroup_coeff(s):
             coeff_grouped = stream.tile([P, CHUNK, PACK], BF16, align_bytes=64)
@@ -248,39 +248,33 @@ def tile_structuredternaryfactorgenerator_pa_t_kernel(
                     in_=coeff_sb[:, 2 * pair : 2 * pair + 2, :],
                 )
 
-        def compute_gains(c):
-            rows = slice(c * CHUNK_TILES, (c + 1) * CHUNK_TILES)
-            gains = stream.tile([P, CHUNK_TILES, O, I], F32)
-            nc.gpsimd.tensor_tensor(
+        def compute_gains(v):
+            rows = slice(2 * v, 2 * v + 2)
+            gains = stream.tile([P, 2, O, I], F32)
+            nc.vector.tensor_tensor(
                 out=gains[:],
-                in0=row_sb[:, rows, :].unsqueeze(3).to_broadcast([P, CHUNK_TILES, O, I]),
-                in1=col_sb[:, rows, :].unsqueeze(2).to_broadcast([P, CHUNK_TILES, O, I]),
+                in0=row_sb[:, rows, :].unsqueeze(3).to_broadcast([P, 2, O, I]),
+                in1=col_sb[:, rows, :].unsqueeze(2).to_broadcast([P, 2, O, I]),
                 op=MULT,
             )
-            gains_tiles[c] = gains
+            gains_tiles[v] = gains
 
-        def stage_2(v, jj):
+        def stage_2(v):
             c, pair = divmod(v, 2)
-            if jj == 0:
-                s2_banks[v] = psum_s2.tile([P, 2, OI], F32, name="s2_bank")
-            s2_bank = s2_banks[v]
-            j = 2 * pair + jj
-            for G in range(K_PASSES):
-                coeff_codes, coeff_scales = coeff_quantised[c * K_PASSES + G]
-                nc.tensor.matmul_mx(
-                    out=s2_bank[:, jj, :],
-                    lhsT=coeff_codes[:, j * P : (j + 1) * P].bitcast(FP8X4),
-                    lhsT_scale=coeff_scales[:, j * P : (j + 1) * P],
-                    rhs=bases_codes[:, G, :].bitcast(FP8X4),
-                    rhs_scale=bases_scales[:, G, :],
-                    start=(G == 0),
-                    stop=(G == K_PASSES - 1),
-                )
-            if jj == 0:
-                return
-            if pair == 0:
-                weight_sb_tiles[c] = stream.tile([P, CHUNK_TILES, OI], F32, name="weight_sb")
-            weight_sb = weight_sb_tiles[c]
+            s2_bank = psum_s2.tile([P, 2, OI], F32)
+            for jj in range(2):
+                j = 2 * pair + jj
+                for G in range(K_PASSES):
+                    coeff_codes, coeff_scales = coeff_quantised[c * K_PASSES + G]
+                    nc.tensor.matmul_mx(
+                        out=s2_bank[:, jj, :],
+                        lhsT=coeff_codes[:, j * P : (j + 1) * P].bitcast(FP8X4),
+                        lhsT_scale=coeff_scales[:, j * P : (j + 1) * P],
+                        rhs=bases_codes[:, G, :].bitcast(FP8X4),
+                        rhs_scale=bases_scales[:, G, :],
+                        start=(G == 0),
+                        stop=(G == K_PASSES - 1),
+                    )
             summed = stream.tile([P, 2, OI], F32)
             nc.vector.tensor_tensor(
                 out=summed[:],
@@ -288,11 +282,17 @@ def tile_structuredternaryfactorgenerator_pa_t_kernel(
                 in1=base_all[:].unsqueeze(1).to_broadcast([P, 2, OI]),
                 op=ADD,
             )
-            js = slice(2 * pair, 2 * pair + 2)
-            nc.gpsimd.tensor_tensor(
-                out=weight_sb[:, js, :],
-                in0=summed[:],
-                in1=gains_tiles[c][:].rearrange("p j o i -> p j (o i)")[:, js, :],
+            summed_tiles[v] = summed
+
+        def scale_weight(v):
+            c, pair = divmod(v, 2)
+            if pair == 0:
+                weight_sb_tiles[c] = stream.tile([P, CHUNK_TILES, OI], F32, name="weight_sb")
+            weight_sb = weight_sb_tiles[c]
+            nc.vector.tensor_tensor(
+                out=weight_sb[:, 2 * pair : 2 * pair + 2, :],
+                in0=summed_tiles[v][:],
+                in1=gains_tiles[v][:].rearrange("p j o i -> p j (o i)"),
                 op=MULT,
             )
             if pair == 1:
@@ -300,36 +300,40 @@ def tile_structuredternaryfactorgenerator_pa_t_kernel(
                     out=weight_rows[:, c * CHUNK_TILES : (c + 1) * CHUNK_TILES, :], in_=weight_sb[:]
                 )
 
+        def is_step(s):
+            return 0 <= s < STEPS
+
         def step(s):
-            has_previous = 1 <= s <= STEPS
             if s % 2 == 0 and s // 2 + 3 < CHUNKS:
                 load_hk(s // 2 + 3)
-            if s % 2 == 1 and s // 2 < CHUNKS:
-                compute_gains(s // 2)
-            if has_previous:
+            if is_step(s - 1):
                 regroup_coeff(s - 1)
+            if is_step(s - STAGE_2_LAG - 1):
+                scale_weight(s - STAGE_2_LAG - 1)
             if s + HK_AHEAD - 1 < HK_UNITS:
                 quantise_hk(s + HK_AHEAD - 1)
-            if has_previous:
+            if is_step(s - STAGE_2_LAG):
+                compute_gains(s - STAGE_2_LAG)
+            if is_step(s - 1):
                 quantise_coeff(s - 1)
-            for half in range(2):
-                if has_previous:
-                    transpose_coeff(s - 1, half)
-                if s + HK_AHEAD < HK_UNITS:
-                    transpose_hk(s + HK_AHEAD, half, nc.vector.tensor_copy)
-                if s < STEPS:
-                    stage_1(s, half)
-                if 0 <= s - 2 < STEPS:
-                    stage_2(s - 2, half)
+            if is_step(s - COEFF_OUT_LAG):
+                transpose_coeff(s - COEFF_OUT_LAG, 0)
+            if s + HK_AHEAD < HK_UNITS:
+                transpose_hk(s + HK_AHEAD, nc.vector.tensor_copy)
+            if is_step(s - COEFF_OUT_LAG):
+                transpose_coeff(s - COEFF_OUT_LAG, 1)
+            if is_step(s):
+                stage_1(s)
+            if is_step(s - STAGE_2_LAG):
+                stage_2(s - STAGE_2_LAG)
 
-        quantise_kw(0)
+        quantise_kw(0, (nc.vector.tensor_copy, nc.scalar.copy))
         for unit in range(HK_AHEAD):
-            for pair in range(2):
-                transpose_hk(unit, pair, nc.scalar.copy)
+            transpose_hk(unit, nc.scalar.copy)
         for unit in range(HK_AHEAD - 1):
             quantise_hk(unit)
-        quantise_kw(1)
+        quantise_kw(1, (nc.vector.tensor_copy, nc.vector.tensor_copy))
         step(0)
         prepare_stage_2()
-        for s in range(1, STEPS + 2):
+        for s in range(1, STEPS + STAGE_2_LAG + 2):
             step(s)

@@ -213,7 +213,8 @@ def tile_structuredternaryfactorgenerator_pa_t_kernel(
         def regroup_coeff(s):
             coeff_grouped = stream.tile([P, CHUNK, PACK], BF16, align_bytes=64)
             nc.vector.tensor_copy(
-                out=coeff_grouped[:], in_=coeff_t_tiles[s][:].rearrange("p t b -> p b t")
+                out=coeff_grouped[:].rearrange("p (c i) t -> p c t i", i=4),
+                in_=coeff_t_tiles[s][:].rearrange("p t (c i) -> p c t i", i=4),
             )
             coeff_grouped_tiles[s] = coeff_grouped
 

@@ -158,13 +158,15 @@ def tile_structuredternaryfactorgenerator_pa_t_kernel(
                 in_=bases_grouped[:].rearrange("p G n t -> p (G n t)"),
             )
 
-        def transpose_hk(unit, copy_out):
+        def transpose_hk(unit, copy_out, pairs):
             c, g = divmod(unit, H_PASSES)
             hk_words = hk_tiles[c][:].bitcast(F32)
             words_per_row = H // 2
-            hk_grouped = stream.tile([P, CHUNK * PACK], BF16, align_bytes=64, bufs=HK_AHEAD)
+            if pairs[0] == 0:
+                hk_grouped_tiles[unit] = stream.tile([P, CHUNK * PACK], BF16, name="hk_grouped", align_bytes=64, bufs=HK_AHEAD)
+            hk_grouped = hk_grouped_tiles[unit]
             grouped_words = hk_grouped[:].bitcast(F32).rearrange("p (b u) -> p b u", u=2)
-            for pair in range(CHUNK_TILES // 2):
+            for pair in pairs:
                 hk_bank = psum_hk.tile([P, BANK], F32)
                 for u in range(2):
                     for jj in range(2):
@@ -178,7 +180,6 @@ def tile_structuredternaryfactorgenerator_pa_t_kernel(
                     out=grouped_words[:, 2 * pair * P : (2 * pair + 2) * P, :],
                     in_=hk_bank[:].rearrange("p (u b) -> p b u", u=2),
                 )
-            hk_grouped_tiles[unit] = hk_grouped
 
         def quantise_hk(unit):
             hk_codes = stream.tile([P, CHUNK], U32, align_bytes=64, bufs=4)
@@ -188,10 +189,12 @@ def tile_structuredternaryfactorgenerator_pa_t_kernel(
             )
             hk_quantised[unit] = (hk_codes, hk_scales)
 
-        def stage_1(s):
+        def stage_1(s, ts):
             c, G = divmod(s, K_PASSES)
-            coeff_t = stream.tile([P, PACK, CHUNK], F32, bufs=3)
-            for t in range(PACK):
+            if ts[0] == 0:
+                coeff_t_tiles[s] = stream.tile([P, PACK, CHUNK], F32, name="coeff_t", bufs=3)
+            coeff_t = coeff_t_tiles[s]
+            for t in ts:
                 s1_bank = psum_s1.tile([P, BANK], F32)
                 for g in range(H_PASSES):
                     hk_codes, hk_scales = hk_quantised[c * H_PASSES + g]
@@ -208,7 +211,6 @@ def tile_structuredternaryfactorgenerator_pa_t_kernel(
                 nc.scalar.activation(
                     out=coeff_t[:, t, :], in_=s1_bank[:], func=TANH, bias=kb[:, m : m + 1]
                 )
-            coeff_t_tiles[s] = coeff_t
 
         def regroup_coeff(s):
             coeff_grouped = stream.tile([P, CHUNK, PACK], BF16, align_bytes=64)
@@ -317,20 +319,19 @@ def tile_structuredternaryfactorgenerator_pa_t_kernel(
                 compute_gains(s - STAGE_2_LAG)
             if is_step(s - 1):
                 quantise_coeff(s - 1)
-            if is_step(s - COEFF_OUT_LAG):
-                transpose_coeff(s - COEFF_OUT_LAG, 0)
-            if s + HK_AHEAD < HK_UNITS:
-                transpose_hk(s + HK_AHEAD, nc.vector.tensor_copy)
-            if is_step(s - COEFF_OUT_LAG):
-                transpose_coeff(s - COEFF_OUT_LAG, 1)
-            if is_step(s):
-                stage_1(s)
-            if is_step(s - STAGE_2_LAG):
-                stage_2(s - STAGE_2_LAG)
+            for r in range(2):
+                if is_step(s - COEFF_OUT_LAG):
+                    transpose_coeff(s - COEFF_OUT_LAG, r)
+                if s + HK_AHEAD < HK_UNITS:
+                    transpose_hk(s + HK_AHEAD, nc.vector.tensor_copy, [r])
+                if is_step(s):
+                    stage_1(s, [2 * r, 2 * r + 1])
+                if r == 1 and is_step(s - STAGE_2_LAG):
+                    stage_2(s - STAGE_2_LAG)
 
         quantise_kw(0, (nc.vector.tensor_copy, nc.scalar.copy))
         for unit in range(HK_AHEAD):
-            transpose_hk(unit, nc.scalar.copy)
+            transpose_hk(unit, nc.scalar.copy, [0, 1])
         for unit in range(HK_AHEAD - 1):
             quantise_hk(unit)
         quantise_kw(1, (nc.vector.tensor_copy, nc.vector.tensor_copy))

@@ -58,6 +58,10 @@ def tile_structuredternaryfactorgenerator_pa_t_kernel(
         stack.enter_context(tc.manual_schedule())
 
         hk_tiles = {}
+        hk_banks = {}
+        co_banks = {}
+        s1_banks = {}
+        s2_banks = {}
         hk_grouped_tiles = {}
         hk_quantised = {}
         coeff_t_tiles = {}
@@ -70,44 +74,46 @@ def tile_structuredternaryfactorgenerator_pa_t_kernel(
 
         def load_hk(c):
             hk_sb = stream.tile([P, CHUNK_TILES * H], BF16, bufs=3)
-            nc.sync.dma_start(
-                out=hk_sb[:].rearrange("p (j h) -> p j h", j=CHUNK_TILES),
-                in_=hk_rows[:, c * CHUNK_TILES : (c + 1) * CHUNK_TILES, :],
-            )
+            tiles = 2 if c == 0 else CHUNK_TILES
+            for j in range(0, CHUNK_TILES, tiles):
+                nc.sync.dma_start(
+                    out=hk_sb[:].rearrange("p (j h) -> p j h", j=CHUNK_TILES)[:, j : j + tiles, :],
+                    in_=hk_rows[:, c * CHUNK_TILES + j : c * CHUNK_TILES + j + tiles, :],
+                )
             hk_tiles[c] = hk_sb
 
         kw_raw = setup.tile([P, K_PASSES, H_PASSES * PACK, K_PASS], BF16)
-        kw_view = kw2.rearrange("(a w e) k -> e w a k", w=P, e=2)
+        kw_view = kw2.rearrange("(a w e) k -> w a e k", w=P, e=2)
 
-        def load_kw(G):
-            for e in range(2):
+        def load_kw(G, blocks):
+            for a in blocks:
                 nc.sync.dma_start(
-                    out=kw_raw[:, G, :, :].rearrange("p (a e) k -> p a e k", e=2)[:, :, e, :],
-                    in_=kw_view[e][:, :, G * K_PASS : (G + 1) * K_PASS],
+                    out=kw_raw[:, G, 2 * a : 2 * a + 2, :],
+                    in_=kw_view[:, a, :, G * K_PASS : (G + 1) * K_PASS],
                 )
-
-        load_kw(0)
-        load_hk(0)
-        load_hk(1)
-        load_kw(1)
-        load_hk(2)
 
         kb_rows = setup.tile([P, P], BF16)
         nc.vector.memset(kb_rows[:], 0.0)
-        nc.scalar.dma_start(out=kb_rows[0 : K // P, :], in_=kb2.rearrange("(m p) -> m p", p=P))
-        bases_raw = setup.tile([P, K_PASSES * PACK, OI], BF16)
-        nc.scalar.dma_start(out=bases_raw[:], in_=bases.rearrange("(a p) o i -> p a (o i)", p=P))
         base_row = setup.tile([P, OI], BF16)
         nc.vector.memset(base_row[:], 0.0)
-        nc.scalar.dma_start(out=base_row[0:1, :], in_=base.rearrange("(a o) i -> a (o i)", a=1))
         row_sb = const.tile([P, ROWS_PER_PARTITION, O], BF16)
-        nc.scalar.dma_start(
+        col_sb = const.tile([P, ROWS_PER_PARTITION, I], BF16)
+        bases_raw = setup.tile([P, K_PASSES * PACK, OI], BF16)
+
+        nc.sync.dma_start(out=kb_rows[0 : K // P, :], in_=kb2.rearrange("(m p) -> m p", p=P))
+        nc.sync.dma_start(out=base_row[0:1, :], in_=base.rearrange("(a o) i -> a (o i)", a=1))
+        load_hk(0)
+        load_kw(0, range(4))
+        load_kw(1, range(4))
+        load_hk(1)
+        nc.sync.dma_start(
             out=row_sb[:], in_=row.rearrange("(p j) o -> p j o", j=ROWS_PER_PARTITION)
         )
-        col_sb = const.tile([P, ROWS_PER_PARTITION, I], BF16)
-        nc.scalar.dma_start(
+        nc.sync.dma_start(
             out=col_sb[:], in_=col.rearrange("(p j) i -> p j i", j=ROWS_PER_PARTITION)
         )
+        nc.sync.dma_start(out=bases_raw[:], in_=bases.rearrange("(a p) o i -> p a (o i)", p=P))
+        load_hk(2)
 
         ident = const.tile([P, P], F32)
         make_identity(nc, ident[:])
@@ -120,6 +126,8 @@ def tile_structuredternaryfactorgenerator_pa_t_kernel(
         nc.tensor.transpose(kb_bank[:, 0:P], kb_rows_f32[:], ident[:])
         kb = const.tile([P, K // P], F32)
         nc.vector.tensor_copy(out=kb[:], in_=kb_bank[:, 0 : K // P])
+        warm = setup.tile([P, 1], F32)
+        nc.scalar.activation(out=warm[:], in_=ident[:, 0:1], func=TANH)
 
         kw_codes = const.tile([P, K_PASSES, H_PASSES, K_PASS], U32, align_bytes=64)
         kw_scales = const.tile([P, K_PASSES, H_PASSES, K_PASS], U8, align_bytes=64)
@@ -127,59 +135,70 @@ def tile_structuredternaryfactorgenerator_pa_t_kernel(
         bases_scales = const.tile([P, K_PASSES, OI], U8, align_bytes=64)
         base_all = const.tile([P, OI], F32)
 
-        def quantise_kw(G, copy_of_pass):
-            kw_grouped = setup.tile([P, H_PASSES, K_PASS, PACK], BF16, align_bytes=64, bufs=2)
-            for g in range(H_PASSES):
-                copy_of_pass[g](
-                    out=kw_grouped[:, g, :, :].rearrange("p (c i) t -> p c t i", i=4),
-                    in_=kw_raw[:, G, g * PACK : (g + 1) * PACK, :].rearrange(
+        kw_grouped_tiles = {}
+
+        def regroup_kw(G, g):
+            kw_grouped = setup.tile([P, K_PASS, PACK], BF16, align_bytes=64, bufs=2)
+            nc.vector.tensor_copy(
+                out=kw_grouped[:].rearrange("p (c i) t -> p c t i", i=4),
+                in_=kw_raw[:, G, g * PACK : (g + 1) * PACK, :].rearrange("p t (c i) -> p c t i", i=4),
+            )
+            kw_grouped_tiles[G, g] = kw_grouped
+
+        def quantise_kw(G, g):
+            nc.vector.quantize_mx(
+                out=kw_codes[:, G, g, :].bitcast(FP8X4),
+                scales=kw_scales[:, G, g, :],
+                in_=kw_grouped_tiles[G, g][:].rearrange("p k t -> p (k t)"),
+            )
+
+        base_bank = psum_co.tile([P, BANK], F32, name="co_bank")
+        nc.tensor.matmul(base_bank[:, 0:OI], lhsT=ones[:], rhs=base_row[:], start=True, stop=True)
+        nc.vector.tensor_copy(out=base_all[:], in_=base_bank[:, 0:OI])
+
+        bases_grouped = setup.tile([P, K_PASSES, OI, PACK], BF16, align_bytes=64)
+
+        def regroup_bases():
+            for G in range(K_PASSES):
+                nc.vector.tensor_copy(
+                    out=bases_grouped[:, G, :, :].rearrange("p (c i) t -> p c t i", i=4),
+                    in_=bases_raw[:, G * PACK : (G + 1) * PACK, :].rearrange(
                         "p t (c i) -> p c t i", i=4
                     ),
                 )
-            nc.vector.quantize_mx(
-                out=kw_codes[:, G, :, :].rearrange("p g k -> p (g k)").bitcast(FP8X4),
-                scales=kw_scales[:, G, :, :].rearrange("p g k -> p (g k)"),
-                in_=kw_grouped[:].rearrange("p g k t -> p (g k t)"),
-            )
 
-        def prepare_stage_2():
-            bases_grouped = setup.tile([P, K_PASSES, OI, PACK], BF16, align_bytes=64)
-            nc.scalar.copy(
-                out=bases_grouped[:], in_=bases_raw[:].rearrange("p (G t) n -> p G n t", t=PACK)
-            )
-            base_bank = psum_co.tile([P, BANK], F32, name="co_bank")
-            nc.tensor.matmul(
-                base_bank[:, 0:OI], lhsT=ones[:], rhs=base_row[:], start=True, stop=True
-            )
-            nc.vector.tensor_copy(out=base_all[:], in_=base_bank[:, 0:OI])
+        def quantise_bases():
             nc.vector.quantize_mx(
                 out=bases_codes[:].rearrange("p G n -> p (G n)").bitcast(FP8X4),
                 scales=bases_scales[:].rearrange("p G n -> p (G n)"),
                 in_=bases_grouped[:].rearrange("p G n t -> p (G n t)"),
             )
 
-        def transpose_hk(unit, copy_out, pairs):
+        def transpose_hk(unit, pair):
             c, g = divmod(unit, H_PASSES)
             hk_words = hk_tiles[c][:].bitcast(F32)
             words_per_row = H // 2
-            if pairs[0] == 0:
-                hk_grouped_tiles[unit] = stream.tile([P, CHUNK * PACK], BF16, name="hk_grouped", align_bytes=64, bufs=HK_AHEAD)
-            hk_grouped = hk_grouped_tiles[unit]
-            grouped_words = hk_grouped[:].bitcast(F32).rearrange("p (b u) -> p b u", u=2)
-            for pair in pairs:
-                hk_bank = psum_hk.tile([P, BANK], F32)
-                for u in range(2):
-                    for jj in range(2):
-                        first = (2 * pair + jj) * words_per_row + (2 * g + u) * P
-                        nc.tensor.transpose(
-                            hk_bank[:, (2 * u + jj) * P : (2 * u + jj + 1) * P],
-                            hk_words[:, first : first + P],
-                            ident[:],
-                        )
-                copy_out(
-                    out=grouped_words[:, 2 * pair * P : (2 * pair + 2) * P, :],
-                    in_=hk_bank[:].rearrange("p (u b) -> p b u", u=2),
+            hk_bank = psum_hk.tile([P, BANK], F32)
+            for u in range(2):
+                for jj in range(2):
+                    first = (2 * pair + jj) * words_per_row + (2 * g + u) * P
+                    nc.tensor.transpose(
+                        hk_bank[:, (2 * u + jj) * P : (2 * u + jj + 1) * P],
+                        hk_words[:, first : first + P],
+                        ident[:],
+                    )
+            hk_banks[unit, pair] = hk_bank
+
+        def empty_hk(unit, pair, copy_out):
+            if pair == 0:
+                hk_grouped_tiles[unit] = stream.tile(
+                    [P, CHUNK * PACK], BF16, name="hk_grouped", align_bytes=64, bufs=HK_AHEAD
                 )
+            grouped_words = hk_grouped_tiles[unit][:].bitcast(F32).rearrange("p (b u) -> p b u", u=2)
+            copy_out(
+                out=grouped_words[:, 2 * pair * P : (2 * pair + 2) * P, :],
+                in_=hk_banks[unit, pair][:].rearrange("p (u b) -> p b u", u=2),
+            )
 
         def quantise_hk(unit):
             hk_codes = stream.tile([P, CHUNK], U32, align_bytes=64, bufs=4)
@@ -189,28 +208,29 @@ def tile_structuredternaryfactorgenerator_pa_t_kernel(
             )
             hk_quantised[unit] = (hk_codes, hk_scales)
 
-        def stage_1(s, ts):
+        def stage_1(s, t):
             c, G = divmod(s, K_PASSES)
-            if ts[0] == 0:
-                coeff_t_tiles[s] = stream.tile([P, PACK, CHUNK], F32, name="coeff_t", bufs=3)
-            coeff_t = coeff_t_tiles[s]
-            for t in ts:
-                s1_bank = psum_s1.tile([P, BANK], F32)
-                for g in range(H_PASSES):
-                    hk_codes, hk_scales = hk_quantised[c * H_PASSES + g]
-                    nc.tensor.matmul_mx(
-                        out=s1_bank[:],
-                        lhsT=kw_codes[:, G, g, t * P : (t + 1) * P].bitcast(FP8X4),
-                        lhsT_scale=kw_scales[:, G, g, t * P : (t + 1) * P],
-                        rhs=hk_codes[:].bitcast(FP8X4),
-                        rhs_scale=hk_scales[:],
-                        start=(g == 0),
-                        stop=(g == H_PASSES - 1),
-                    )
-                m = G * PACK + t
-                nc.scalar.activation(
-                    out=coeff_t[:, t, :], in_=s1_bank[:], func=TANH, bias=kb[:, m : m + 1]
+            s1_bank = psum_s1.tile([P, BANK], F32)
+            for g in range(H_PASSES):
+                hk_codes, hk_scales = hk_quantised[c * H_PASSES + g]
+                nc.tensor.matmul_mx(
+                    out=s1_bank[:],
+                    lhsT=kw_codes[:, G, g, t * P : (t + 1) * P].bitcast(FP8X4),
+                    lhsT_scale=kw_scales[:, G, g, t * P : (t + 1) * P],
+                    rhs=hk_codes[:].bitcast(FP8X4),
+                    rhs_scale=hk_scales[:],
+                    start=(g == 0),
+                    stop=(g == H_PASSES - 1),
                 )
+            s1_banks[s, t] = s1_bank
+
+        def tanh(s, t):
+            if t == 0:
+                coeff_t_tiles[s] = stream.tile([P, PACK, CHUNK], F32, name="coeff_t", bufs=3)
+            m = s % K_PASSES * PACK + t
+            nc.scalar.activation(
+                out=coeff_t_tiles[s][:, t, :], in_=s1_banks[s, t][:], func=TANH, bias=kb[:, m : m + 1]
+            )
 
         def regroup_coeff(s):
             coeff_grouped = stream.tile([P, CHUNK, PACK], BF16, align_bytes=64)
@@ -230,25 +250,26 @@ def tile_structuredternaryfactorgenerator_pa_t_kernel(
             )
             coeff_quantised[s] = (coeff_codes, coeff_scales)
 
-        def transpose_coeff(s, pair):
+        def transpose_coeff(s, j):
+            co_bank = psum_co.tile([P, BANK], F32)
+            for t in range(PACK):
+                nc.tensor.transpose(
+                    co_bank[:, t * P : (t + 1) * P],
+                    coeff_t_tiles[s][:, t, j * P : (j + 1) * P],
+                    ident[:],
+                )
+            co_banks[s, j] = co_bank
+
+        def empty_coeff(s, j, copy_out):
             c, G = divmod(s, K_PASSES)
-            if G == 0 and pair == 0:
+            if G == 0 and j == 0:
                 coeff_sb_tiles[c] = stream.tile([P, CHUNK_TILES, K], F32, name="coeff_sb", bufs=3)
             coeff_sb = coeff_sb_tiles[c]
-            for j in range(2 * pair, 2 * pair + 2):
-                co_bank = psum_co.tile([P, BANK], F32)
-                for t in range(PACK):
-                    nc.tensor.transpose(
-                        co_bank[:, t * P : (t + 1) * P],
-                        coeff_t_tiles[s][:, t, j * P : (j + 1) * P],
-                        ident[:],
-                    )
-                nc.scalar.copy(out=coeff_sb[:, j, G * BANK : (G + 1) * BANK], in_=co_bank[:])
-            if G == K_PASSES - 1:
-                first = c * CHUNK_TILES + 2 * pair
+            copy_out(out=coeff_sb[:, j, G * BANK : (G + 1) * BANK], in_=co_banks[s, j][:])
+            if G == K_PASSES - 1 and j % 2 == 1:
+                first = c * CHUNK_TILES + j - 1
                 nc.sync.dma_start(
-                    out=coeff_rows[:, first : first + 2, :],
-                    in_=coeff_sb[:, 2 * pair : 2 * pair + 2, :],
+                    out=coeff_rows[:, first : first + 2, :], in_=coeff_sb[:, j - 1 : j + 1, :]
                 )
 
         def compute_gains(v):
@@ -278,10 +299,13 @@ def tile_structuredternaryfactorgenerator_pa_t_kernel(
                         start=(G == 0),
                         stop=(G == K_PASSES - 1),
                     )
+            s2_banks[v] = s2_bank
+
+        def add_base(v):
             summed = stream.tile([P, 2, OI], F32)
             nc.vector.tensor_tensor(
                 out=summed[:],
-                in0=s2_bank[:],
+                in0=s2_banks[v][:],
                 in1=base_all[:].unsqueeze(1).to_broadcast([P, 2, OI]),
                 op=ADD,
             )
@@ -306,36 +330,66 @@ def tile_structuredternaryfactorgenerator_pa_t_kernel(
         def is_step(s):
             return 0 <= s < STEPS
 
-        def step(s):
+        def step(s, units, quantise_first, quantise_last):
+            copy_v = nc.vector.tensor_copy
+            copy_s = nc.scalar.copy
+            done = s - COEFF_OUT_LAG
+            v = s - STAGE_2_LAG
             if s % 2 == 0 and s // 2 + 3 < CHUNKS:
                 load_hk(s // 2 + 3)
-            if is_step(s - 1):
-                regroup_coeff(s - 1)
-            if is_step(s - STAGE_2_LAG - 1):
-                scale_weight(s - STAGE_2_LAG - 1)
-            if s + HK_AHEAD - 1 < HK_UNITS:
-                quantise_hk(s + HK_AHEAD - 1)
-            if is_step(s - STAGE_2_LAG):
-                compute_gains(s - STAGE_2_LAG)
-            if is_step(s - 1):
-                quantise_coeff(s - 1)
+            for unit in quantise_first:
+                quantise_hk(unit)
             for r in range(2):
-                if is_step(s - COEFF_OUT_LAG):
-                    transpose_coeff(s - COEFF_OUT_LAG, r)
-                if s + HK_AHEAD < HK_UNITS:
-                    transpose_hk(s + HK_AHEAD, nc.vector.tensor_copy, [r])
+                for j in (2 * r, 2 * r + 1):
+                    if is_step(done):
+                        transpose_coeff(done, j)
+                        empty_coeff(done, j, copy_s)
+                if s >= 2:
+                    for unit in units:
+                        transpose_hk(unit, r)
+                        empty_hk(unit, r, copy_v if s > 2 and (r == 0 or s % 2) else copy_s)
                 if is_step(s):
-                    stage_1(s, [2 * r, 2 * r + 1])
-                if r == 1 and is_step(s - STAGE_2_LAG):
-                    stage_2(s - STAGE_2_LAG)
+                    for t in (2 * r, 2 * r + 1):
+                        stage_1(s, t)
+                        tanh(s, t)
+                if s < 2:
+                    for unit in units:
+                        transpose_hk(unit, r)
+                        empty_hk(unit, r, copy_s)
+                if r == 0:
+                    if is_step(s - 1):
+                        regroup_coeff(s - 1)
+                    if is_step(v):
+                        compute_gains(v)
+                    if is_step(v):
+                        stage_2(v)
+                        add_base(v)
+                if r == 1:
+                    if is_step(s - 1):
+                        quantise_coeff(s - 1)
+                    if is_step(v):
+                        scale_weight(v)
+            for unit in quantise_last:
+                quantise_hk(unit)
 
-        quantise_kw(0, (nc.vector.tensor_copy, nc.scalar.copy))
-        for unit in range(HK_AHEAD):
-            transpose_hk(unit, nc.scalar.copy, [0, 1])
-        for unit in range(HK_AHEAD - 1):
-            quantise_hk(unit)
-        quantise_kw(1, (nc.vector.tensor_copy, nc.vector.tensor_copy))
-        step(0)
-        prepare_stage_2()
-        for s in range(1, STEPS + STAGE_2_LAG + 2):
-            step(s)
+        for pair in range(2):
+            for unit, copy_out in ((0, nc.scalar.copy), (1, nc.vector.tensor_copy)):
+                transpose_hk(unit, pair)
+                empty_hk(unit, pair, copy_out)
+        regroup_kw(0, 0)
+        quantise_hk(0)
+        quantise_kw(0, 0)
+        regroup_kw(0, 1)
+        quantise_hk(1)
+        quantise_kw(0, 1)
+        step(0, [2], [], [])
+        for g in range(2):
+            regroup_kw(1, g)
+        for g in range(2):
+            quantise_kw(1, g)
+        step(1, [3], [2], [3])
+        regroup_bases()
+        step(2, [4, 5], [], [4])
+        quantise_bases()
+        for s in range(3, STEPS + STAGE_2_LAG + 1):
+            step(s, [s + 3] if s + 3 < HK_UNITS else [], [s + 2] if s + 2 < HK_UNITS else [], [])

@@ -28,7 +28,9 @@ K_PASSES = K // K_PASS
 ROWS_PER_PARTITION = B // P
 CHUNK_TILES = 4
 CHUNK = CHUNK_TILES * P
-CHUNKS = B // CHUNK
+PAIRS = (2, 2, 2, 2, 2, 2, 2, 2)
+FIRST_PAIR = [sum(PAIRS[:c]) for c in range(len(PAIRS))]
+CHUNKS = len(PAIRS)
 STEPS = CHUNKS * K_PASSES
 HK_UNITS = CHUNKS * H_PASSES
 HK_AHEAD = 3
@@ -74,11 +76,12 @@ def tile_structuredternaryfactorgenerator_pa_t_kernel(
 
         def load_hk(c):
             hk_sb = stream.tile([P, CHUNK_TILES * H], BF16, bufs=3)
-            tiles = 2 if c == 0 else CHUNK_TILES
-            for j in range(0, CHUNK_TILES, tiles):
+            tiles = 2 if c == 0 else 2 * PAIRS[c]
+            for j in range(0, 2 * PAIRS[c], tiles):
+                first = 2 * FIRST_PAIR[c] + j
                 nc.sync.dma_start(
                     out=hk_sb[:].rearrange("p (j h) -> p j h", j=CHUNK_TILES)[:, j : j + tiles, :],
-                    in_=hk_rows[:, c * CHUNK_TILES + j : c * CHUNK_TILES + j + tiles, :],
+                    in_=hk_rows[:, first : first + tiles, :],
                 )
             hk_tiles[c] = hk_sb
 
@@ -137,9 +140,9 @@ def tile_structuredternaryfactorgenerator_pa_t_kernel(
 
         kw_grouped_tiles = {}
 
-        def regroup_kw(G, g):
+        def regroup_kw(G, g, copy_out):
             kw_grouped = setup.tile([P, K_PASS, PACK], BF16, align_bytes=64, bufs=2)
-            nc.vector.tensor_copy(
+            copy_out(
                 out=kw_grouped[:].rearrange("p (c i) t -> p c t i", i=4),
                 in_=kw_raw[:, G, g * PACK : (g + 1) * PACK, :].rearrange("p t (c i) -> p c t i", i=4),
             )
@@ -174,6 +177,9 @@ def tile_structuredternaryfactorgenerator_pa_t_kernel(
                 in_=bases_grouped[:].rearrange("p G n t -> p (G n t)"),
             )
 
+        def samples(s):
+            return PAIRS[s // 2] * 2 * P
+
         def transpose_hk(unit, pair):
             c, g = divmod(unit, H_PASSES)
             hk_words = hk_tiles[c][:].bitcast(F32)
@@ -203,22 +209,26 @@ def tile_structuredternaryfactorgenerator_pa_t_kernel(
         def quantise_hk(unit):
             hk_codes = stream.tile([P, CHUNK], U32, align_bytes=64, bufs=4)
             hk_scales = stream.tile([P, CHUNK], U8, align_bytes=64, bufs=4)
+            n = samples(unit)
             nc.vector.quantize_mx(
-                out=hk_codes[:].bitcast(FP8X4), scales=hk_scales[:], in_=hk_grouped_tiles[unit][:]
+                out=hk_codes[:, 0:n].bitcast(FP8X4),
+                scales=hk_scales[:, 0:n],
+                in_=hk_grouped_tiles[unit][:, 0 : n * PACK],
             )
             hk_quantised[unit] = (hk_codes, hk_scales)
 
         def stage_1(s, t):
             c, G = divmod(s, K_PASSES)
+            n = samples(s)
             s1_bank = psum_s1.tile([P, BANK], F32)
             for g in range(H_PASSES):
                 hk_codes, hk_scales = hk_quantised[c * H_PASSES + g]
                 nc.tensor.matmul_mx(
-                    out=s1_bank[:],
+                    out=s1_bank[:, 0:n],
                     lhsT=kw_codes[:, G, g, t * P : (t + 1) * P].bitcast(FP8X4),
                     lhsT_scale=kw_scales[:, G, g, t * P : (t + 1) * P],
-                    rhs=hk_codes[:].bitcast(FP8X4),
-                    rhs_scale=hk_scales[:],
+                    rhs=hk_codes[:, 0:n].bitcast(FP8X4),
+                    rhs_scale=hk_scales[:, 0:n],
                     start=(g == 0),
                     stop=(g == H_PASSES - 1),
                 )
@@ -228,25 +238,31 @@ def tile_structuredternaryfactorgenerator_pa_t_kernel(
             if t == 0:
                 coeff_t_tiles[s] = stream.tile([P, PACK, CHUNK], F32, name="coeff_t", bufs=3)
             m = s % K_PASSES * PACK + t
+            n = samples(s)
             nc.scalar.activation(
-                out=coeff_t_tiles[s][:, t, :], in_=s1_banks[s, t][:], func=TANH, bias=kb[:, m : m + 1]
+                out=coeff_t_tiles[s][:, t, 0:n],
+                in_=s1_banks[s, t][:, 0:n],
+                func=TANH,
+                bias=kb[:, m : m + 1],
             )
 
         def regroup_coeff(s):
             coeff_grouped = stream.tile([P, CHUNK, PACK], BF16, align_bytes=64)
+            n = samples(s)
             nc.vector.tensor_copy(
-                out=coeff_grouped[:].rearrange("p (c i) t -> p c t i", i=4),
-                in_=coeff_t_tiles[s][:].rearrange("p t (c i) -> p c t i", i=4),
+                out=coeff_grouped[:, 0:n, :].rearrange("p (c i) t -> p c t i", i=4),
+                in_=coeff_t_tiles[s][:, :, 0:n].rearrange("p t (c i) -> p c t i", i=4),
             )
             coeff_grouped_tiles[s] = coeff_grouped
 
         def quantise_coeff(s):
             coeff_codes = stream.tile([P, CHUNK], U32, align_bytes=64, bufs=4)
             coeff_scales = stream.tile([P, CHUNK], U8, align_bytes=64, bufs=4)
+            n = samples(s)
             nc.vector.quantize_mx(
-                out=coeff_codes[:].bitcast(FP8X4),
-                scales=coeff_scales[:],
-                in_=coeff_grouped_tiles[s][:].rearrange("p b t -> p (b t)"),
+                out=coeff_codes[:, 0:n].bitcast(FP8X4),
+                scales=coeff_scales[:, 0:n],
+                in_=coeff_grouped_tiles[s][:, 0:n, :].rearrange("p b t -> p (b t)"),
             )
             coeff_quantised[s] = (coeff_codes, coeff_scales)
 
@@ -262,19 +278,21 @@ def tile_structuredternaryfactorgenerator_pa_t_kernel(
 
         def empty_coeff(s, j, copy_out):
             c, G = divmod(s, K_PASSES)
-            if G == 0 and j == 0:
-                coeff_sb_tiles[c] = stream.tile([P, CHUNK_TILES, K], F32, name="coeff_sb", bufs=3)
-            coeff_sb = coeff_sb_tiles[c]
-            copy_out(out=coeff_sb[:, j, G * BANK : (G + 1) * BANK], in_=co_banks[s, j][:])
-            if G == K_PASSES - 1 and j % 2 == 1:
-                first = c * CHUNK_TILES + j - 1
+            if j % 2 == 0:
+                coeff_sb_tiles[s, j // 2] = stream.tile(
+                    [P, 2, BANK], F32, name="coeff_sb", bufs=8
+                )
+            coeff_sb = coeff_sb_tiles[s, j // 2]
+            copy_out(out=coeff_sb[:, j % 2, :], in_=co_banks[s, j][:])
+            if j % 2 == 1:
+                first = 2 * FIRST_PAIR[c] + j - 1
                 nc.sync.dma_start(
-                    out=coeff_rows[:, first : first + 2, :], in_=coeff_sb[:, j - 1 : j + 1, :]
+                    out=coeff_rows[:, first : first + 2, G * BANK : (G + 1) * BANK], in_=coeff_sb[:]
                 )
 
         def compute_gains(v):
             rows = slice(2 * v, 2 * v + 2)
-            gains = stream.tile([P, 2, O, I], F32)
+            gains = stream.tile([P, 2, O, I], F32, bufs=4)
             nc.vector.tensor_tensor(
                 out=gains[:],
                 in0=row_sb[:, rows, :].unsqueeze(3).to_broadcast([P, 2, O, I]),
@@ -284,7 +302,8 @@ def tile_structuredternaryfactorgenerator_pa_t_kernel(
             gains_tiles[v] = gains
 
         def stage_2(v):
-            c, pair = divmod(v, 2)
+            c = max(c for c in range(CHUNKS) if FIRST_PAIR[c] <= v)
+            pair = v - FIRST_PAIR[c]
             s2_bank = psum_s2.tile([P, 2, OI], F32)
             for jj in range(2):
                 j = 2 * pair + jj
@@ -312,84 +331,106 @@ def tile_structuredternaryfactorgenerator_pa_t_kernel(
             summed_tiles[v] = summed
 
         def scale_weight(v):
-            c, pair = divmod(v, 2)
-            if pair == 0:
-                weight_sb_tiles[c] = stream.tile([P, CHUNK_TILES, OI], F32, name="weight_sb")
-            weight_sb = weight_sb_tiles[c]
+            weight_sb = stream.tile([P, 2, OI], F32, bufs=4)
             nc.vector.tensor_tensor(
-                out=weight_sb[:, 2 * pair : 2 * pair + 2, :],
+                out=weight_sb[:],
                 in0=summed_tiles[v][:],
                 in1=gains_tiles[v][:].rearrange("p j o i -> p j (o i)"),
                 op=MULT,
             )
-            if pair == 1:
-                nc.sync.dma_start(
-                    out=weight_rows[:, c * CHUNK_TILES : (c + 1) * CHUNK_TILES, :], in_=weight_sb[:]
-                )
+            nc.sync.dma_start(out=weight_rows[:, 2 * v : 2 * v + 2, :], in_=weight_sb[:])
 
         def is_step(s):
             return 0 <= s < STEPS
 
-        def step(s, units, quantise_first, quantise_last):
-            copy_v = nc.vector.tensor_copy
-            copy_s = nc.scalar.copy
-            done = s - COEFF_OUT_LAG
-            v = s - STAGE_2_LAG
+        copy_v = nc.vector.tensor_copy
+        copy_s = nc.scalar.copy
+
+        def coeff_out(s, half, copies):
+            if is_step(s):
+                n = PAIRS[s // 2]
+                for j, copy_out in zip(range(half * n, half * n + n), copies):
+                    transpose_coeff(s, j)
+                    empty_coeff(s, j, copy_out)
+
+        def stage_2_pairs(s):
+            c, second = divmod(s - 2, 2)
+            return [FIRST_PAIR[c] + second] if 0 <= c < CHUNKS and second < PAIRS[c] else []
+
+        def step(s):
+            unit = s + 2
             if s % 2 == 0 and s // 2 + 3 < CHUNKS:
                 load_hk(s // 2 + 3)
-            for unit in quantise_first:
-                quantise_hk(unit)
             for r in range(2):
-                for j in (2 * r, 2 * r + 1):
-                    if is_step(done):
-                        transpose_coeff(done, j)
-                        empty_coeff(done, j, copy_s)
-                if s >= 2:
-                    for unit in units:
-                        transpose_hk(unit, r)
-                        empty_hk(unit, r, copy_v if s > 2 and (r == 0 or s % 2) else copy_s)
-                if is_step(s):
-                    for t in (2 * r, 2 * r + 1):
-                        stage_1(s, t)
-                        tanh(s, t)
-                if s < 2:
-                    for unit in units:
-                        transpose_hk(unit, r)
-                        empty_hk(unit, r, copy_s)
+                if 0 < s and unit < HK_UNITS and r < PAIRS[unit // 2]:
+                    transpose_hk(unit, r)
+                    if r == 0:
+                        empty_hk(unit, 0, copy_s)
+                coeff_out(s - 2 + r, 1 - r, (copy_s, copy_s))
+                for t in (2 * r, 2 * r + 1):
+                    stage_1(s, t)
+                    tanh(s, t)
                 if r == 0:
+                    for v in stage_2_pairs(s - 1):
+                        add_base(v)
                     if is_step(s - 1):
                         regroup_coeff(s - 1)
-                    if is_step(v):
-                        compute_gains(v)
-                    if is_step(v):
-                        stage_2(v)
-                        add_base(v)
-                if r == 1:
+                    for v in stage_2_pairs(s - 1):
+                        scale_weight(v)
                     if is_step(s - 1):
                         quantise_coeff(s - 1)
-                    if is_step(v):
-                        scale_weight(v)
-            for unit in quantise_last:
-                quantise_hk(unit)
+                if r == 1:
+                    for v in stage_2_pairs(s):
+                        stage_2(v)
+                    if s == 0:
+                        for rr in range(2):
+                            transpose_hk(unit, rr)
+                            empty_hk(unit, rr, copy_s)
+                    elif unit < HK_UNITS and PAIRS[unit // 2] == 2:
+                        empty_hk(unit, 1, copy_v)
+                    if s == 0:
+                        for g in range(2):
+                            regroup_kw(1, g, copy_v)
+                        for g in range(2):
+                            quantise_kw(1, g)
+                    for v in stage_2_pairs(s + 1):
+                        compute_gains(v)
+                    if unit < HK_UNITS:
+                        quantise_hk(unit)
+                    if s == 1:
+                        regroup_bases()
+                        quantise_bases()
+
+        def tail():
+            last = STEPS - 1
+            coeff_out(last - 1, 1, (copy_s, copy_s))
+            regroup_coeff(last)
+            for v in stage_2_pairs(last):
+                add_base(v)
+            quantise_coeff(last)
+            for v in stage_2_pairs(last):
+                scale_weight(v)
+            coeff_out(last, 0, (copy_s, copy_s))
+            ending = stage_2_pairs(last + 1) + stage_2_pairs(last + 2)
+            for v in ending:
+                stage_2(v)
+            coeff_out(last, 1, (copy_s, copy_s))
+            compute_gains(ending[1])
+            for v in ending:
+                add_base(v)
+            for v in ending:
+                scale_weight(v)
 
         for pair in range(2):
-            for unit, copy_out in ((0, nc.scalar.copy), (1, nc.vector.tensor_copy)):
+            for unit in range(2):
                 transpose_hk(unit, pair)
-                empty_hk(unit, pair, copy_out)
-        regroup_kw(0, 0)
-        quantise_hk(0)
+                empty_hk(unit, pair, copy_s)
+        regroup_kw(0, 0, copy_v)
+        regroup_kw(0, 1, copy_s)
         quantise_kw(0, 0)
-        regroup_kw(0, 1)
+        quantise_hk(0)
         quantise_hk(1)
         quantise_kw(0, 1)
-        step(0, [2], [], [])
-        for g in range(2):
-            regroup_kw(1, g)
-        for g in range(2):
-            quantise_kw(1, g)
-        step(1, [3], [2], [3])
-        regroup_bases()
-        step(2, [4, 5], [], [4])
-        quantise_bases()
-        for s in range(3, STEPS + STAGE_2_LAG + 1):
-            step(s, [s + 3] if s + 3 < HK_UNITS else [], [s + 2] if s + 2 < HK_UNITS else [], [])
+        for s in range(STEPS):
+            step(s)
+        tail()

@@ -122,6 +122,13 @@ def tile_structuredternaryfactorgenerator_pa_t_kernel(
         make_identity(nc, ident[:])
         ones = const.tile([P, P], BF16)
         nc.vector.memset(ones[:], 1.0)
+        zeros = const.tile([P, BANK], BF16)
+        nc.vector.memset(zeros[:], 0.0)
+
+        def keep_clock(n):
+            s1_bank = psum_s1.tile([P, BANK], F32)
+            for i in range(n):
+                nc.tensor.matmul(s1_bank[:], lhsT=ones[:], rhs=zeros[:], start=True, stop=True)
 
         kb_rows_f32 = setup.tile([P, P], F32)
         nc.vector.tensor_copy(out=kb_rows_f32[:], in_=kb_rows[:])
@@ -246,25 +253,27 @@ def tile_structuredternaryfactorgenerator_pa_t_kernel(
                 bias=kb[:, m : m + 1],
             )
 
-        def regroup_coeff(s):
-            coeff_grouped = stream.tile([P, CHUNK, PACK], BF16, align_bytes=64)
-            n = samples(s)
+        def regroup_coeff(s, cols):
+            if cols.start == 0:
+                coeff_grouped_tiles[s] = stream.tile(
+                    [P, CHUNK, PACK], BF16, name="coeff_grouped", align_bytes=64
+                )
             nc.vector.tensor_copy(
-                out=coeff_grouped[:, 0:n, :].rearrange("p (c i) t -> p c t i", i=4),
-                in_=coeff_t_tiles[s][:, :, 0:n].rearrange("p t (c i) -> p c t i", i=4),
+                out=coeff_grouped_tiles[s][:, cols, :].rearrange("p (c i) t -> p c t i", i=4),
+                in_=coeff_t_tiles[s][:, :, cols].rearrange("p t (c i) -> p c t i", i=4),
             )
-            coeff_grouped_tiles[s] = coeff_grouped
 
-        def quantise_coeff(s):
-            coeff_codes = stream.tile([P, CHUNK], U32, align_bytes=64, bufs=4)
-            coeff_scales = stream.tile([P, CHUNK], U8, align_bytes=64, bufs=4)
-            n = samples(s)
+        def quantise_coeff(s, cols):
+            if cols.start == 0:
+                coeff_codes = stream.tile([P, CHUNK], U32, align_bytes=64, bufs=4)
+                coeff_scales = stream.tile([P, CHUNK], U8, align_bytes=64, bufs=4)
+                coeff_quantised[s] = (coeff_codes, coeff_scales)
+            coeff_codes, coeff_scales = coeff_quantised[s]
             nc.vector.quantize_mx(
-                out=coeff_codes[:, 0:n].bitcast(FP8X4),
-                scales=coeff_scales[:, 0:n],
-                in_=coeff_grouped_tiles[s][:, 0:n, :].rearrange("p b t -> p (b t)"),
+                out=coeff_codes[:, cols].bitcast(FP8X4),
+                scales=coeff_scales[:, cols],
+                in_=coeff_grouped_tiles[s][:, cols, :].rearrange("p b t -> p (b t)"),
             )
-            coeff_quantised[s] = (coeff_codes, coeff_scales)
 
         def transpose_coeff(s, j):
             co_bank = psum_co.tile([P, BANK], F32)
@@ -343,58 +352,60 @@ def tile_structuredternaryfactorgenerator_pa_t_kernel(
         def is_step(s):
             return 0 <= s < STEPS
 
+        ALL = slice(0, CHUNK)
         copy_v = nc.vector.tensor_copy
         copy_s = nc.scalar.copy
 
-        def coeff_out(s, half, copies):
+        def coeff_out(s, half):
             if is_step(s):
-                n = PAIRS[s // 2]
-                for j, copy_out in zip(range(half * n, half * n + n), copies):
+                for j in (2 * half, 2 * half + 1):
                     transpose_coeff(s, j)
-                    empty_coeff(s, j, copy_out)
-
-        def stage_2_pairs(s):
-            c, second = divmod(s - 2, 2)
-            return [FIRST_PAIR[c] + second] if 0 <= c < CHUNKS and second < PAIRS[c] else []
+                    empty_coeff(s, j, copy_s)
 
         def step(s):
             unit = s + 2
-            if s % 2 == 0 and s // 2 + 3 < CHUNKS:
+            even = s % 2 == 0
+            v = s - 2 if even else s - 3
+            if even and s // 2 + 3 < CHUNKS:
                 load_hk(s // 2 + 3)
             for r in range(2):
-                if 0 < s and unit < HK_UNITS and r < PAIRS[unit // 2]:
+                if 0 < s and unit < HK_UNITS:
                     transpose_hk(unit, r)
                     if r == 0:
-                        empty_hk(unit, 0, copy_s)
-                coeff_out(s - 2 + r, 1 - r, (copy_s, copy_s))
+                        empty_hk(unit, 0, copy_v if s % 2 == 0 else copy_s)
+                coeff_out(s - 2 + r, 1 - r)
                 for t in (2 * r, 2 * r + 1):
                     stage_1(s, t)
                     tanh(s, t)
+                if 0 <= v and r == (1 if even else 0):
+                    stage_2(v + (0 if even else 1))
+                if s == 0 and r == 1:
+                    for rr in range(2):
+                        transpose_hk(unit, rr)
+                        empty_hk(unit, rr, copy_s)
                 if r == 0:
-                    for v in stage_2_pairs(s - 1):
+                    if not even and 0 <= v:
                         add_base(v)
                     if is_step(s - 1):
-                        regroup_coeff(s - 1)
-                    for v in stage_2_pairs(s - 1):
-                        scale_weight(v)
+                        regroup_coeff(s - 1, ALL)
+                    if 0 <= (v if not even else v - 1):
+                        scale_weight(v if not even else v - 1)
                     if is_step(s - 1):
-                        quantise_coeff(s - 1)
+                        quantise_coeff(s - 1, ALL)
                 if r == 1:
-                    for v in stage_2_pairs(s):
-                        stage_2(v)
-                    if s == 0:
-                        for rr in range(2):
-                            transpose_hk(unit, rr)
-                            empty_hk(unit, rr, copy_s)
-                    elif unit < HK_UNITS and PAIRS[unit // 2] == 2:
+                    if 0 < s and unit < HK_UNITS:
                         empty_hk(unit, 1, copy_v)
                     if s == 0:
                         for g in range(2):
                             regroup_kw(1, g, copy_v)
                         for g in range(2):
                             quantise_kw(1, g)
-                    for v in stage_2_pairs(s + 1):
-                        compute_gains(v)
+                    if 0 <= v:
+                        if even:
+                            compute_gains(v)
+                            compute_gains(v + 1)
+                        else:
+                            add_base(v + 1)
                     if unit < HK_UNITS:
                         quantise_hk(unit)
                     if s == 1:
@@ -403,28 +414,33 @@ def tile_structuredternaryfactorgenerator_pa_t_kernel(
 
         def tail():
             last = STEPS - 1
-            coeff_out(last - 1, 1, (copy_s, copy_s))
-            regroup_coeff(last)
-            for v in stage_2_pairs(last):
-                add_base(v)
-            quantise_coeff(last)
-            for v in stage_2_pairs(last):
-                scale_weight(v)
-            coeff_out(last, 0, (copy_s, copy_s))
-            ending = stage_2_pairs(last + 1) + stage_2_pairs(last + 2)
-            for v in ending:
-                stage_2(v)
-            coeff_out(last, 1, (copy_s, copy_s))
-            compute_gains(ending[1])
-            for v in ending:
-                add_base(v)
-            for v in ending:
-                scale_weight(v)
+            v = STEPS - 2
+            low = slice(0, CHUNK // 2)
+            high = slice(CHUNK // 2, CHUNK)
+            compute_gains(v)
+            compute_gains(v + 1)
+            coeff_out(last - 1, 1)
+            keep_clock(2)
+            regroup_coeff(last, low)
+            regroup_coeff(last, high)
+            quantise_coeff(last, low)
+            scale_weight(v - 1)
+            quantise_coeff(last, high)
+            coeff_out(last, 0)
+            keep_clock(1)
+            coeff_out(last, 1)
+            stage_2(v)
+            stage_2(v + 1)
+            add_base(v)
+            add_base(v + 1)
+            scale_weight(v)
+            scale_weight(v + 1)
 
         for pair in range(2):
             for unit in range(2):
                 transpose_hk(unit, pair)
                 empty_hk(unit, pair, copy_s)
+        keep_clock(4)
         regroup_kw(0, 0, copy_v)
         regroup_kw(0, 1, copy_s)
         quantise_kw(0, 0)

@@ -28,9 +28,7 @@ K_PASSES = K // K_PASS
 ROWS_PER_PARTITION = B // P
 CHUNK_TILES = 4
 CHUNK = CHUNK_TILES * P
-PAIRS = (2, 2, 2, 2, 2, 2, 2, 2)
-FIRST_PAIR = [sum(PAIRS[:c]) for c in range(len(PAIRS))]
-CHUNKS = len(PAIRS)
+CHUNKS = B // CHUNK
 STEPS = CHUNKS * K_PASSES
 HK_UNITS = CHUNKS * H_PASSES
 HK_AHEAD = 3
@@ -74,16 +72,14 @@ def tile_structuredternaryfactorgenerator_pa_t_kernel(
         weight_sb_tiles = {}
         summed_tiles = {}
 
-        def load_hk(c):
-            hk_sb = stream.tile([P, CHUNK_TILES * H], BF16, bufs=3)
-            tiles = 2 if c == 0 else 2 * PAIRS[c]
-            for j in range(0, 2 * PAIRS[c], tiles):
-                first = 2 * FIRST_PAIR[c] + j
+        def load_hk(c, tiles=CHUNK_TILES):
+            if c not in hk_tiles:
+                hk_tiles[c] = stream.tile([P, CHUNK_TILES, H], BF16, name="hk_sb", bufs=3)
+            for j in range(0, CHUNK_TILES, tiles):
+                first = c * CHUNK_TILES + j
                 nc.sync.dma_start(
-                    out=hk_sb[:].rearrange("p (j h) -> p j h", j=CHUNK_TILES)[:, j : j + tiles, :],
-                    in_=hk_rows[:, first : first + tiles, :],
+                    out=hk_tiles[c][:, j : j + tiles, :], in_=hk_rows[:, first : first + tiles, :]
                 )
-            hk_tiles[c] = hk_sb
 
         kw_raw = setup.tile([P, K_PASSES, H_PASSES * PACK, K_PASS], BF16)
         kw_view = kw2.rearrange("(a w e) k -> w a e k", w=P, e=2)
@@ -95,6 +91,10 @@ def tile_structuredternaryfactorgenerator_pa_t_kernel(
                     in_=kw_view[:, a, :, G * K_PASS : (G + 1) * K_PASS],
                 )
 
+        ones = const.tile([P, P], BF16)
+        nc.vector.memset(ones[:], 1.0)
+        zeros = const.tile([P, BANK], BF16)
+        nc.gpsimd.memset(zeros[:], 0.0)
         kb_rows = setup.tile([P, P], BF16)
         nc.vector.memset(kb_rows[:], 0.0)
         base_row = setup.tile([P, OI], BF16)
@@ -103,10 +103,11 @@ def tile_structuredternaryfactorgenerator_pa_t_kernel(
         col_sb = const.tile([P, ROWS_PER_PARTITION, I], BF16)
         bases_raw = setup.tile([P, K_PASSES * PACK, OI], BF16)
 
+        load_kw(0, (0, 1))
+        load_hk(0, 2)
         nc.sync.dma_start(out=kb_rows[0 : K // P, :], in_=kb2.rearrange("(m p) -> m p", p=P))
         nc.sync.dma_start(out=base_row[0:1, :], in_=base.rearrange("(a o) i -> a (o i)", a=1))
-        load_hk(0)
-        load_kw(0, range(4))
+        load_kw(0, (2, 3))
         load_kw(1, range(4))
         load_hk(1)
         nc.sync.dma_start(
@@ -120,22 +121,23 @@ def tile_structuredternaryfactorgenerator_pa_t_kernel(
 
         ident = const.tile([P, P], F32)
         make_identity(nc, ident[:])
-        ones = const.tile([P, P], BF16)
-        nc.vector.memset(ones[:], 1.0)
-        zeros = const.tile([P, BANK], BF16)
-        nc.vector.memset(zeros[:], 0.0)
 
         def keep_clock(n):
             s1_bank = psum_s1.tile([P, BANK], F32)
             for i in range(n):
                 nc.tensor.matmul(s1_bank[:], lhsT=ones[:], rhs=zeros[:], start=True, stop=True)
 
-        kb_rows_f32 = setup.tile([P, P], F32)
-        nc.vector.tensor_copy(out=kb_rows_f32[:], in_=kb_rows[:])
-        kb_bank = psum_co.tile([P, BANK], F32, name="co_bank")
-        nc.tensor.transpose(kb_bank[:, 0:P], kb_rows_f32[:], ident[:])
+        keep_clock(5)
+
         kb = const.tile([P, K // P], F32)
-        nc.vector.tensor_copy(out=kb[:], in_=kb_bank[:, 0 : K // P])
+
+        def prepare_bias():
+            kb_rows_f32 = setup.tile([P, P], F32)
+            nc.scalar.copy(out=kb_rows_f32[:], in_=kb_rows[:])
+            kb_bank = psum_co.tile([P, BANK], F32, name="co_bank")
+            nc.tensor.transpose(kb_bank[:, 0:P], kb_rows_f32[:], ident[:])
+            nc.scalar.copy(out=kb[:], in_=kb_bank[:, 0 : K // P])
+
         warm = setup.tile([P, 1], F32)
         nc.scalar.activation(out=warm[:], in_=ident[:, 0:1], func=TANH)
 
@@ -147,13 +149,17 @@ def tile_structuredternaryfactorgenerator_pa_t_kernel(
 
         kw_grouped_tiles = {}
 
-        def regroup_kw(G, g, copy_out):
-            kw_grouped = setup.tile([P, K_PASS, PACK], BF16, align_bytes=64, bufs=2)
+        def regroup_kw(G, g, cols, copy_out):
+            if (G, g) not in kw_grouped_tiles:
+                kw_grouped_tiles[G, g] = setup.tile(
+                    [P, K_PASS, PACK], BF16, name="kw_grouped", align_bytes=64, bufs=2
+                )
             copy_out(
-                out=kw_grouped[:].rearrange("p (c i) t -> p c t i", i=4),
-                in_=kw_raw[:, G, g * PACK : (g + 1) * PACK, :].rearrange("p t (c i) -> p c t i", i=4),
+                out=kw_grouped_tiles[G, g][:, cols, :].rearrange("p (c i) t -> p c t i", i=4),
+                in_=kw_raw[:, G, g * PACK : (g + 1) * PACK, cols].rearrange(
+                    "p t (c i) -> p c t i", i=4
+                ),
             )
-            kw_grouped_tiles[G, g] = kw_grouped
 
         def quantise_kw(G, g):
             nc.vector.quantize_mx(
@@ -162,9 +168,13 @@ def tile_structuredternaryfactorgenerator_pa_t_kernel(
                 in_=kw_grouped_tiles[G, g][:].rearrange("p k t -> p (k t)"),
             )
 
-        base_bank = psum_co.tile([P, BANK], F32, name="co_bank")
-        nc.tensor.matmul(base_bank[:, 0:OI], lhsT=ones[:], rhs=base_row[:], start=True, stop=True)
-        nc.vector.tensor_copy(out=base_all[:], in_=base_bank[:, 0:OI])
+        def spread_base():
+            base_bank = psum_co.tile([P, BANK], F32, name="co_bank")
+            nc.tensor.matmul(
+                base_bank[:, 0:OI], lhsT=ones[:], rhs=base_row[:], start=True, stop=True
+            )
+            nc.scalar.copy(out=base_all[:], in_=base_bank[:, 0:OI])
+
 
         bases_grouped = setup.tile([P, K_PASSES, OI, PACK], BF16, align_bytes=64)
 
@@ -184,14 +194,14 @@ def tile_structuredternaryfactorgenerator_pa_t_kernel(
                 in_=bases_grouped[:].rearrange("p G n t -> p (G n t)"),
             )
 
-        def samples(s):
-            return PAIRS[s // 2] * 2 * P
-
         def transpose_hk(unit, pair):
             c, g = divmod(unit, H_PASSES)
-            hk_words = hk_tiles[c][:].bitcast(F32)
+            hk_words = hk_tiles[c][:].rearrange("p j h -> p (j h)").bitcast(F32)
             words_per_row = H // 2
-            hk_bank = psum_hk.tile([P, BANK], F32)
+            if unit < 2 and pair == 1:
+                hk_bank = psum_co.tile([P, BANK], F32, name="co_bank")
+            else:
+                hk_bank = psum_hk.tile([P, BANK], F32)
             for u in range(2):
                 for jj in range(2):
                     first = (2 * pair + jj) * words_per_row + (2 * g + u) * P
@@ -216,39 +226,36 @@ def tile_structuredternaryfactorgenerator_pa_t_kernel(
         def quantise_hk(unit):
             hk_codes = stream.tile([P, CHUNK], U32, align_bytes=64, bufs=4)
             hk_scales = stream.tile([P, CHUNK], U8, align_bytes=64, bufs=4)
-            n = samples(unit)
             nc.vector.quantize_mx(
-                out=hk_codes[:, 0:n].bitcast(FP8X4),
-                scales=hk_scales[:, 0:n],
-                in_=hk_grouped_tiles[unit][:, 0 : n * PACK],
+                out=hk_codes[:].bitcast(FP8X4),
+                scales=hk_scales[:],
+                in_=hk_grouped_tiles[unit][:],
             )
             hk_quantised[unit] = (hk_codes, hk_scales)
 
-        def stage_1(s, t):
+        def stage_1(s, t, passes=range(H_PASSES)):
             c, G = divmod(s, K_PASSES)
-            n = samples(s)
-            s1_bank = psum_s1.tile([P, BANK], F32)
-            for g in range(H_PASSES):
+            if passes[0] == 0:
+                s1_banks[s, t] = psum_s1.tile([P, BANK], F32, name="s1_bank")
+            for g in passes:
                 hk_codes, hk_scales = hk_quantised[c * H_PASSES + g]
                 nc.tensor.matmul_mx(
-                    out=s1_bank[:, 0:n],
+                    out=s1_banks[s, t][:],
                     lhsT=kw_codes[:, G, g, t * P : (t + 1) * P].bitcast(FP8X4),
                     lhsT_scale=kw_scales[:, G, g, t * P : (t + 1) * P],
-                    rhs=hk_codes[:, 0:n].bitcast(FP8X4),
-                    rhs_scale=hk_scales[:, 0:n],
+                    rhs=hk_codes[:].bitcast(FP8X4),
+                    rhs_scale=hk_scales[:],
                     start=(g == 0),
                     stop=(g == H_PASSES - 1),
                 )
-            s1_banks[s, t] = s1_bank
 
         def tanh(s, t):
             if t == 0:
                 coeff_t_tiles[s] = stream.tile([P, PACK, CHUNK], F32, name="coeff_t", bufs=3)
             m = s % K_PASSES * PACK + t
-            n = samples(s)
             nc.scalar.activation(
-                out=coeff_t_tiles[s][:, t, 0:n],
-                in_=s1_banks[s, t][:, 0:n],
+                out=coeff_t_tiles[s][:, t, :],
+                in_=s1_banks[s, t][:],
                 func=TANH,
                 bias=kb[:, m : m + 1],
             )
@@ -294,26 +301,29 @@ def tile_structuredternaryfactorgenerator_pa_t_kernel(
             coeff_sb = coeff_sb_tiles[s, j // 2]
             copy_out(out=coeff_sb[:, j % 2, :], in_=co_banks[s, j][:])
             if j % 2 == 1:
-                first = 2 * FIRST_PAIR[c] + j - 1
+                first = c * CHUNK_TILES + j - 1
                 nc.sync.dma_start(
                     out=coeff_rows[:, first : first + 2, G * BANK : (G + 1) * BANK], in_=coeff_sb[:]
                 )
 
-        def compute_gains(v):
-            rows = slice(2 * v, 2 * v + 2)
-            gains = stream.tile([P, 2, O, I], F32, bufs=4)
+        def compute_gains(c):
+            rows = slice(c * CHUNK_TILES, (c + 1) * CHUNK_TILES)
+            shape = [P, CHUNK_TILES, O, I]
+            gains = stream.tile(shape, F32)
             nc.vector.tensor_tensor(
                 out=gains[:],
-                in0=row_sb[:, rows, :].unsqueeze(3).to_broadcast([P, 2, O, I]),
-                in1=col_sb[:, rows, :].unsqueeze(2).to_broadcast([P, 2, O, I]),
+                in0=row_sb[:, rows, :].unsqueeze(3).to_broadcast(shape),
+                in1=col_sb[:, rows, :].unsqueeze(2).to_broadcast(shape),
                 op=MULT,
             )
-            gains_tiles[v] = gains
+            gains_tiles[c] = gains
 
         def stage_2(v):
-            c = max(c for c in range(CHUNKS) if FIRST_PAIR[c] <= v)
-            pair = v - FIRST_PAIR[c]
-            s2_bank = psum_s2.tile([P, 2, OI], F32)
+            c, pair = divmod(v, 2)
+            if v == B // (2 * P) - 1:
+                s2_bank = psum_s1.tile([P, 2, OI], F32, name="s1_bank")
+            else:
+                s2_bank = psum_s2.tile([P, 2, OI], F32)
             for jj in range(2):
                 j = 2 * pair + jj
                 for G in range(K_PASSES):
@@ -330,29 +340,39 @@ def tile_structuredternaryfactorgenerator_pa_t_kernel(
             s2_banks[v] = s2_bank
 
         def add_base(v):
-            summed = stream.tile([P, 2, OI], F32)
+            c, pair = divmod(v, 2)
+            if pair == 0:
+                summed_tiles[c] = stream.tile([P, CHUNK_TILES, OI], F32, name="summed")
             nc.vector.tensor_tensor(
-                out=summed[:],
+                out=summed_tiles[c][:, 2 * pair : 2 * pair + 2, :],
                 in0=s2_banks[v][:],
                 in1=base_all[:].unsqueeze(1).to_broadcast([P, 2, OI]),
                 op=ADD,
             )
-            summed_tiles[v] = summed
 
-        def scale_weight(v):
-            weight_sb = stream.tile([P, 2, OI], F32, bufs=4)
+        def scale_weight(c, tiles):
+            if tiles.start == 0:
+                weight_sb_tiles[c] = stream.tile([P, CHUNK_TILES, OI], F32, name="weight_sb")
+            weight_sb = weight_sb_tiles[c]
             nc.vector.tensor_tensor(
-                out=weight_sb[:],
-                in0=summed_tiles[v][:],
-                in1=gains_tiles[v][:].rearrange("p j o i -> p j (o i)"),
+                out=weight_sb[:, tiles, :],
+                in0=summed_tiles[c][:, tiles, :],
+                in1=gains_tiles[c][:, tiles, :, :].rearrange("p j o i -> p j (o i)"),
                 op=MULT,
             )
-            nc.sync.dma_start(out=weight_rows[:, 2 * v : 2 * v + 2, :], in_=weight_sb[:])
+            nc.sync.dma_start(
+                out=weight_rows[
+                    :, c * CHUNK_TILES + tiles.start : c * CHUNK_TILES + tiles.stop, :
+                ],
+                in_=weight_sb[:, tiles, :],
+            )
 
         def is_step(s):
             return 0 <= s < STEPS
 
         ALL = slice(0, CHUNK)
+        LOW = slice(0, CHUNK // 2)
+        HIGH = slice(CHUNK // 2, CHUNK)
         copy_v = nc.vector.tensor_copy
         copy_s = nc.scalar.copy
 
@@ -369,41 +389,32 @@ def tile_structuredternaryfactorgenerator_pa_t_kernel(
             if even and s // 2 + 3 < CHUNKS:
                 load_hk(s // 2 + 3)
             for r in range(2):
-                if 0 < s and unit < HK_UNITS:
+                if unit < HK_UNITS and (1 < s or r == 1):
                     transpose_hk(unit, r)
                     if r == 0:
-                        empty_hk(unit, 0, copy_v if s % 2 == 0 else copy_s)
+                        empty_hk(unit, 0, copy_v if s % 4 == 1 and 1 < s else copy_s)
                 coeff_out(s - 2 + r, 1 - r)
                 for t in (2 * r, 2 * r + 1):
                     stage_1(s, t)
                     tanh(s, t)
+                if s == 1 and r == 0:
+                    transpose_hk(unit, 0)
+                    empty_hk(unit, 0, copy_s)
                 if 0 <= v and r == (1 if even else 0):
                     stage_2(v + (0 if even else 1))
-                if s == 0 and r == 1:
-                    for rr in range(2):
-                        transpose_hk(unit, rr)
-                        empty_hk(unit, rr, copy_s)
                 if r == 0:
                     if not even and 0 <= v:
                         add_base(v)
-                    if is_step(s - 1):
-                        regroup_coeff(s - 1, ALL)
-                    if 0 <= (v if not even else v - 1):
-                        scale_weight(v if not even else v - 1)
-                    if is_step(s - 1):
-                        quantise_coeff(s - 1, ALL)
+                    regroup_coeff(s - 1, ALL)
+                    if even and 0 < v:
+                        scale_weight(v // 2 - 1, slice(0, CHUNK_TILES))
+                    quantise_coeff(s - 1, ALL)
                 if r == 1:
-                    if 0 < s and unit < HK_UNITS:
+                    if unit < HK_UNITS:
                         empty_hk(unit, 1, copy_v)
-                    if s == 0:
-                        for g in range(2):
-                            regroup_kw(1, g, copy_v)
-                        for g in range(2):
-                            quantise_kw(1, g)
                     if 0 <= v:
                         if even:
-                            compute_gains(v)
-                            compute_gains(v + 1)
+                            compute_gains(v // 2)
                         else:
                             add_base(v + 1)
                     if unit < HK_UNITS:
@@ -412,41 +423,63 @@ def tile_structuredternaryfactorgenerator_pa_t_kernel(
                         regroup_bases()
                         quantise_bases()
 
+        def first_step():
+            regroup_kw(0, 0, ALL, copy_v)
+            quantise_kw(0, 0)
+            for pair in range(2):
+                for unit in range(2):
+                    transpose_hk(unit, pair)
+                    empty_hk(unit, pair, (copy_s, copy_v)[unit])
+            keep_clock(2)
+            regroup_kw(0, 1, LOW, copy_v)
+            regroup_kw(0, 1, HIGH, copy_s)
+            prepare_bias()
+            spread_base()
+            quantise_hk(0)
+            quantise_hk(1)
+            quantise_kw(0, 1)
+            for t in range(3):
+                stage_1(0, t, (0,))
+            regroup_kw(1, 1, HIGH, copy_s)
+            regroup_kw(1, 0, ALL, copy_v)
+            regroup_kw(1, 1, LOW, copy_v)
+            for t in range(3):
+                stage_1(0, t, (1,))
+                tanh(0, t)
+            stage_1(0, 3)
+            tanh(0, 3)
+            quantise_kw(1, 0)
+            quantise_kw(1, 1)
+            for pair in range(2):
+                transpose_hk(2, pair)
+                empty_hk(2, pair, copy_s)
+            quantise_hk(2)
+            load_hk(3)
+
         def tail():
             last = STEPS - 1
             v = STEPS - 2
-            low = slice(0, CHUNK // 2)
-            high = slice(CHUNK // 2, CHUNK)
-            compute_gains(v)
-            compute_gains(v + 1)
+            scale_weight(CHUNKS - 2, slice(0, CHUNK_TILES))
+            compute_gains(CHUNKS - 1)
             coeff_out(last - 1, 1)
             keep_clock(2)
-            regroup_coeff(last, low)
-            regroup_coeff(last, high)
-            quantise_coeff(last, low)
-            scale_weight(v - 1)
-            quantise_coeff(last, high)
+            regroup_coeff(last, LOW)
+            regroup_coeff(last, HIGH)
+            quantise_coeff(last, LOW)
+            quantise_coeff(last, HIGH)
             coeff_out(last, 0)
-            keep_clock(1)
-            coeff_out(last, 1)
             stage_2(v)
+            transpose_coeff(last, 2)
+            empty_coeff(last, 2, copy_s)
             stage_2(v + 1)
+            transpose_coeff(last, 3)
+            empty_coeff(last, 3, copy_s)
             add_base(v)
             add_base(v + 1)
-            scale_weight(v)
-            scale_weight(v + 1)
+            scale_weight(CHUNKS - 1, slice(0, 2))
+            scale_weight(CHUNKS - 1, slice(2, 4))
 
-        for pair in range(2):
-            for unit in range(2):
-                transpose_hk(unit, pair)
-                empty_hk(unit, pair, copy_s)
-        keep_clock(4)
-        regroup_kw(0, 0, copy_v)
-        regroup_kw(0, 1, copy_s)
-        quantise_kw(0, 0)
-        quantise_hk(0)
-        quantise_hk(1)
-        quantise_kw(0, 1)
-        for s in range(STEPS):
+        first_step()
+        for s in range(1, STEPS):
             step(s)
         tail()

@@ -233,29 +233,29 @@ def tile_structuredternaryfactorgenerator_pa_t_kernel(
             )
             hk_quantised[unit] = (hk_codes, hk_scales)
 
-        def stage_1(s, t, passes=range(H_PASSES)):
+        def stage_1(s, t, passes=range(H_PASSES), cols=slice(0, CHUNK)):
             c, G = divmod(s, K_PASSES)
             if passes[0] == 0:
                 s1_banks[s, t] = psum_s1.tile([P, BANK], F32, name="s1_bank")
             for g in passes:
                 hk_codes, hk_scales = hk_quantised[c * H_PASSES + g]
                 nc.tensor.matmul_mx(
-                    out=s1_banks[s, t][:],
+                    out=s1_banks[s, t][:, cols],
                     lhsT=kw_codes[:, G, g, t * P : (t + 1) * P].bitcast(FP8X4),
                     lhsT_scale=kw_scales[:, G, g, t * P : (t + 1) * P],
-                    rhs=hk_codes[:].bitcast(FP8X4),
-                    rhs_scale=hk_scales[:],
+                    rhs=hk_codes[:, cols].bitcast(FP8X4),
+                    rhs_scale=hk_scales[:, cols],
                     start=(g == 0),
                     stop=(g == H_PASSES - 1),
                 )
 
-        def tanh(s, t):
-            if t == 0:
+        def tanh(s, t, cols=slice(0, CHUNK)):
+            if t == 0 and cols.start == 0:
                 coeff_t_tiles[s] = stream.tile([P, PACK, CHUNK], F32, name="coeff_t", bufs=3)
             m = s % K_PASSES * PACK + t
             nc.scalar.activation(
-                out=coeff_t_tiles[s][:, t, :],
-                in_=s1_banks[s, t][:],
+                out=coeff_t_tiles[s][:, t, cols],
+                in_=s1_banks[s, t][:, cols],
                 func=TANH,
                 bias=kb[:, m : m + 1],
             )
@@ -309,7 +309,7 @@ def tile_structuredternaryfactorgenerator_pa_t_kernel(
         def compute_gains(c):
             rows = slice(c * CHUNK_TILES, (c + 1) * CHUNK_TILES)
             shape = [P, CHUNK_TILES, O, I]
-            gains = stream.tile(shape, F32)
+            gains = stream.tile(shape, F32, bufs=4)
             nc.vector.tensor_tensor(
                 out=gains[:],
                 in0=row_sb[:, rows, :].unsqueeze(3).to_broadcast(shape),
@@ -367,61 +367,72 @@ def tile_structuredternaryfactorgenerator_pa_t_kernel(
                 in_=weight_sb[:, tiles, :],
             )
 
-        def is_step(s):
-            return 0 <= s < STEPS
-
+        GAINS_STEP = {3: 0, 5: 1, 7: 2, 9: 3, 11: 4, 12: 5, 13: 6}
         ALL = slice(0, CHUNK)
         LOW = slice(0, CHUNK // 2)
         HIGH = slice(CHUNK // 2, CHUNK)
         copy_v = nc.vector.tensor_copy
         copy_s = nc.scalar.copy
 
-        def coeff_out(s, half):
-            if is_step(s):
-                for j in (2 * half, 2 * half + 1):
-                    transpose_coeff(s, j)
-                    empty_coeff(s, j, copy_s)
+        def coeff_out(s, tiles, copies):
+            for j, copy_out in zip(tiles, copies):
+                transpose_coeff(s, j)
+                empty_coeff(s, j, copy_out)
 
         def step(s):
-            unit = s + 2
             even = s % 2 == 0
-            v = s - 2 if even else s - 3
+            units = {1: [3, 4], 2: [5]}.get(s, [s + 3] if s + 3 < HK_UNITS else [])
+            v = s - 3
             if even and s // 2 + 3 < CHUNKS:
                 load_hk(s // 2 + 3)
+            if 2 < s and s + 2 < HK_UNITS:
+                quantise_hk(s + 2)
+            if s == STEPS - 1:
+                stage_2(v)
+                add_base(v)
             for r in range(2):
-                if unit < HK_UNITS and (1 < s or r == 1):
-                    transpose_hk(unit, r)
-                    if r == 0:
-                        empty_hk(unit, 0, copy_v if s % 4 == 1 and 1 < s else copy_s)
-                coeff_out(s - 2 + r, 1 - r)
+                if 2 <= s:
+                    coeff_out(s - 2, (2 * r, 2 * r + 1), (copy_s, copy_s))
+                if 2 <= s:
+                    for unit in units:
+                        transpose_hk(unit, r)
                 for t in (2 * r, 2 * r + 1):
                     stage_1(s, t)
                     tanh(s, t)
-                if s == 1 and r == 0:
-                    transpose_hk(unit, 0)
-                    empty_hk(unit, 0, copy_s)
-                if 0 <= v and r == (1 if even else 0):
-                    stage_2(v + (0 if even else 1))
+                if s == 1:
+                    for pair in range(2):
+                        transpose_hk(units[r], pair)
+                        empty_hk(units[r], pair, (copy_s, copy_v)[pair])
+                    quantise_hk(units[r])
                 if r == 0:
-                    if not even and 0 <= v:
+                    if 2 <= s:
+                        for unit in units:
+                            empty_hk(unit, 0, copy_v)
+                        regroup_coeff(s - 1, ALL)
+                    if s in GAINS_STEP:
+                        compute_gains(GAINS_STEP[s])
+                    if 0 <= v < STEPS - 4:
+                        stage_2(v)
                         add_base(v)
-                    regroup_coeff(s - 1, ALL)
-                    if even and 0 < v:
-                        scale_weight(v // 2 - 1, slice(0, CHUNK_TILES))
-                    quantise_coeff(s - 1, ALL)
+                    if s == STEPS - 1:
+                        stage_2(v + 1)
+                        quantise_coeff(s - 1, ALL)
+                        add_base(v + 1)
                 if r == 1:
-                    if unit < HK_UNITS:
-                        empty_hk(unit, 1, copy_v)
-                    if 0 <= v:
-                        if even:
-                            compute_gains(v // 2)
-                        else:
-                            add_base(v + 1)
-                    if unit < HK_UNITS:
-                        quantise_hk(unit)
+                    if 2 <= s:
+                        for unit in units:
+                            empty_hk(unit, 1, copy_v if even else copy_s)
                     if s == 1:
+                        regroup_coeff(0, ALL)
                         regroup_bases()
+                    if s < STEPS - 1:
+                        quantise_coeff(s - 1, ALL)
+                    if s == 1:
                         quantise_bases()
+                    if 0 < v and (even or s == STEPS - 1):
+                        scale_weight(v // 2, slice(0, CHUNK_TILES))
+                    if s == STEPS - 2:
+                        compute_gains(CHUNKS - 1)
 
         def first_step():
             regroup_kw(0, 0, ALL, copy_v)
@@ -459,24 +470,20 @@ def tile_structuredternaryfactorgenerator_pa_t_kernel(
         def tail():
             last = STEPS - 1
             v = STEPS - 2
-            scale_weight(CHUNKS - 2, slice(0, CHUNK_TILES))
-            compute_gains(CHUNKS - 1)
-            coeff_out(last - 1, 1)
-            keep_clock(2)
+            coeff_out(last - 1, (0, 1), (copy_s, copy_s))
+            keep_clock(3)
+            coeff_out(last - 1, (2, 3), (copy_s, copy_s))
             regroup_coeff(last, LOW)
             regroup_coeff(last, HIGH)
             quantise_coeff(last, LOW)
             quantise_coeff(last, HIGH)
-            coeff_out(last, 0)
             stage_2(v)
-            transpose_coeff(last, 2)
-            empty_coeff(last, 2, copy_s)
+            coeff_out(last, (0, 1), (copy_s, copy_s))
             stage_2(v + 1)
-            transpose_coeff(last, 3)
-            empty_coeff(last, 3, copy_s)
+            coeff_out(last, (2, 3), (copy_s, copy_s))
             add_base(v)
-            add_base(v + 1)
             scale_weight(CHUNKS - 1, slice(0, 2))
+            add_base(v + 1)
             scale_weight(CHUNKS - 1, slice(2, 4))
 
         first_step()

@@ -29,10 +29,10 @@ ROWS_PER_PARTITION = B // P
 CHUNK_TILES = 4
 CHUNK = CHUNK_TILES * P
 CHUNKS = B // CHUNK
+PAIRS = B // (2 * P)
 STEPS = CHUNKS * K_PASSES
 HK_UNITS = CHUNKS * H_PASSES
 HK_AHEAD = 3
-COEFF_OUT_LAG = 2
 STAGE_2_LAG = 3
 
 FLOPS = 2 * B * H * K + 2 * B * K * OI
@@ -69,17 +69,24 @@ def tile_structuredternaryfactorgenerator_pa_t_kernel(
         coeff_quantised = {}
         coeff_sb_tiles = {}
         gains_tiles = {}
-        weight_sb_tiles = {}
         summed_tiles = {}
 
-        def load_hk(c, tiles=CHUNK_TILES):
+        def load_hk(c, features=slice(0, H)):
             if c not in hk_tiles:
-                hk_tiles[c] = stream.tile([P, CHUNK_TILES, H], BF16, name="hk_sb", bufs=3)
-            for j in range(0, CHUNK_TILES, tiles):
-                first = c * CHUNK_TILES + j
-                nc.sync.dma_start(
-                    out=hk_tiles[c][:, j : j + tiles, :], in_=hk_rows[:, first : first + tiles, :]
-                )
+                hk_tiles[c] = stream.tile([P, CHUNK_TILES, H], BF16, name="hk_sb", bufs=4)
+            first = c * CHUNK_TILES
+            nc.sync.dma_start(
+                out=hk_tiles[c][:, :, features],
+                in_=hk_rows[:, first : first + CHUNK_TILES, features],
+            )
+
+        def load_gains():
+            nc.sync.dma_start(
+                out=row_sb[:], in_=row.rearrange("(p j) o -> p j o", j=ROWS_PER_PARTITION)
+            )
+            nc.sync.dma_start(
+                out=col_sb[:], in_=col.rearrange("(p j) i -> p j i", j=ROWS_PER_PARTITION)
+            )
 
         kw_raw = setup.tile([P, K_PASSES, H_PASSES * PACK, K_PASS], BF16)
         kw_view = kw2.rearrange("(a w e) k -> w a e k", w=P, e=2)
@@ -103,21 +110,20 @@ def tile_structuredternaryfactorgenerator_pa_t_kernel(
         col_sb = const.tile([P, ROWS_PER_PARTITION, I], BF16)
         bases_raw = setup.tile([P, K_PASSES * PACK, OI], BF16)
 
+        first_half = slice(0, K_PASS)
+        second_half = slice(K_PASS, H)
         load_kw(0, (0, 1))
-        load_hk(0, 2)
+        load_hk(0, first_half)
         nc.sync.dma_start(out=kb_rows[0 : K // P, :], in_=kb2.rearrange("(m p) -> m p", p=P))
-        nc.sync.dma_start(out=base_row[0:1, :], in_=base.rearrange("(a o) i -> a (o i)", a=1))
         load_kw(0, (2, 3))
+        load_hk(0, second_half)
         load_kw(1, range(4))
-        load_hk(1)
-        nc.sync.dma_start(
-            out=row_sb[:], in_=row.rearrange("(p j) o -> p j o", j=ROWS_PER_PARTITION)
-        )
-        nc.sync.dma_start(
-            out=col_sb[:], in_=col.rearrange("(p j) i -> p j i", j=ROWS_PER_PARTITION)
-        )
-        nc.sync.dma_start(out=bases_raw[:], in_=bases.rearrange("(a p) o i -> p a (o i)", p=P))
+        load_hk(1, first_half)
+        load_hk(1, second_half)
+        nc.sync.dma_start(out=base_row[0:1, :], in_=base.rearrange("(a o) i -> a (o i)", a=1))
         load_hk(2)
+        nc.sync.dma_start(out=bases_raw[:], in_=bases.rearrange("(a p) o i -> p a (o i)", p=P))
+        load_hk(3)
 
         ident = const.tile([P, P], F32)
         make_identity(nc, ident[:])
@@ -127,7 +133,7 @@ def tile_structuredternaryfactorgenerator_pa_t_kernel(
             for i in range(n):
                 nc.tensor.matmul(s1_bank[:], lhsT=ones[:], rhs=zeros[:], start=True, stop=True)
 
-        keep_clock(5)
+        keep_clock(9)
 
         kb = const.tile([P, K // P], F32)
 
@@ -152,7 +158,7 @@ def tile_structuredternaryfactorgenerator_pa_t_kernel(
         def regroup_kw(G, g, cols, copy_out):
             if (G, g) not in kw_grouped_tiles:
                 kw_grouped_tiles[G, g] = setup.tile(
-                    [P, K_PASS, PACK], BF16, name="kw_grouped", align_bytes=64, bufs=2
+                    [P, K_PASS, PACK], BF16, name="kw_grouped", align_bytes=64, bufs=4
                 )
             copy_out(
                 out=kw_grouped_tiles[G, g][:, cols, :].rearrange("p (c i) t -> p c t i", i=4),
@@ -169,7 +175,7 @@ def tile_structuredternaryfactorgenerator_pa_t_kernel(
             )
 
         def spread_base():
-            base_bank = psum_co.tile([P, BANK], F32, name="co_bank")
+            base_bank = psum_s2.tile([P, BANK], F32, name="s2_bank")
             nc.tensor.matmul(
                 base_bank[:, 0:OI], lhsT=ones[:], rhs=base_row[:], start=True, stop=True
             )
@@ -198,7 +204,7 @@ def tile_structuredternaryfactorgenerator_pa_t_kernel(
             c, g = divmod(unit, H_PASSES)
             hk_words = hk_tiles[c][:].rearrange("p j h -> p (j h)").bitcast(F32)
             words_per_row = H // 2
-            if unit < 2 and pair == 1:
+            if unit == 1:
                 hk_bank = psum_co.tile([P, BANK], F32, name="co_bank")
             else:
                 hk_bank = psum_hk.tile([P, BANK], F32)
@@ -215,7 +221,7 @@ def tile_structuredternaryfactorgenerator_pa_t_kernel(
         def empty_hk(unit, pair, copy_out):
             if pair == 0:
                 hk_grouped_tiles[unit] = stream.tile(
-                    [P, CHUNK * PACK], BF16, name="hk_grouped", align_bytes=64, bufs=HK_AHEAD
+                    [P, CHUNK * PACK], BF16, name="hk_grouped", align_bytes=64, bufs=4
                 )
             grouped_words = hk_grouped_tiles[unit][:].bitcast(F32).rearrange("p (b u) -> p b u", u=2)
             copy_out(
@@ -224,8 +230,8 @@ def tile_structuredternaryfactorgenerator_pa_t_kernel(
             )
 
         def quantise_hk(unit):
-            hk_codes = stream.tile([P, CHUNK], U32, align_bytes=64, bufs=4)
-            hk_scales = stream.tile([P, CHUNK], U8, align_bytes=64, bufs=4)
+            hk_codes = stream.tile([P, CHUNK], U32, align_bytes=64, bufs=7)
+            hk_scales = stream.tile([P, CHUNK], U8, align_bytes=64, bufs=7)
             nc.vector.quantize_mx(
                 out=hk_codes[:].bitcast(FP8X4),
                 scales=hk_scales[:],
@@ -236,7 +242,12 @@ def tile_structuredternaryfactorgenerator_pa_t_kernel(
         def stage_1(s, t, passes=range(H_PASSES), cols=slice(0, CHUNK)):
             c, G = divmod(s, K_PASSES)
             if passes[0] == 0:
-                s1_banks[s, t] = psum_s1.tile([P, BANK], F32, name="s1_bank")
+                if s == 0 and t == PACK - 1:
+                    s1_banks[s, t] = psum_co.tile([P, BANK], F32, name="co_bank")
+                elif s == 1 and t == PACK - 1:
+                    s1_banks[s, t] = psum_s2.tile([P, BANK], F32, name="s2_bank")
+                else:
+                    s1_banks[s, t] = psum_s1.tile([P, BANK], F32, name="s1_bank")
             for g in passes:
                 hk_codes, hk_scales = hk_quantised[c * H_PASSES + g]
                 nc.tensor.matmul_mx(
@@ -251,7 +262,7 @@ def tile_structuredternaryfactorgenerator_pa_t_kernel(
 
         def tanh(s, t, cols=slice(0, CHUNK)):
             if t == 0 and cols.start == 0:
-                coeff_t_tiles[s] = stream.tile([P, PACK, CHUNK], F32, name="coeff_t", bufs=3)
+                coeff_t_tiles[s] = stream.tile([P, PACK, CHUNK], F32, name="coeff_t", bufs=4)
             m = s % K_PASSES * PACK + t
             nc.scalar.activation(
                 out=coeff_t_tiles[s][:, t, cols],
@@ -272,8 +283,8 @@ def tile_structuredternaryfactorgenerator_pa_t_kernel(
 
         def quantise_coeff(s, cols):
             if cols.start == 0:
-                coeff_codes = stream.tile([P, CHUNK], U32, align_bytes=64, bufs=4)
-                coeff_scales = stream.tile([P, CHUNK], U8, align_bytes=64, bufs=4)
+                coeff_codes = stream.tile([P, CHUNK], U32, align_bytes=64, bufs=6)
+                coeff_scales = stream.tile([P, CHUNK], U8, align_bytes=64, bufs=6)
                 coeff_quantised[s] = (coeff_codes, coeff_scales)
             coeff_codes, coeff_scales = coeff_quantised[s]
             nc.vector.quantize_mx(
@@ -296,7 +307,7 @@ def tile_structuredternaryfactorgenerator_pa_t_kernel(
             c, G = divmod(s, K_PASSES)
             if j % 2 == 0:
                 coeff_sb_tiles[s, j // 2] = stream.tile(
-                    [P, 2, BANK], F32, name="coeff_sb", bufs=8
+                    [P, 2, BANK], F32, name="coeff_sb", bufs=6
                 )
             coeff_sb = coeff_sb_tiles[s, j // 2]
             copy_out(out=coeff_sb[:, j % 2, :], in_=co_banks[s, j][:])
@@ -306,22 +317,22 @@ def tile_structuredternaryfactorgenerator_pa_t_kernel(
                     out=coeff_rows[:, first : first + 2, G * BANK : (G + 1) * BANK], in_=coeff_sb[:]
                 )
 
-        def compute_gains(c):
-            rows = slice(c * CHUNK_TILES, (c + 1) * CHUNK_TILES)
-            shape = [P, CHUNK_TILES, O, I]
-            gains = stream.tile(shape, F32, bufs=4)
-            nc.vector.tensor_tensor(
+        def compute_gains(v):
+            rows = slice(2 * v, 2 * v + 2)
+            shape = [P, 2, O, I]
+            gains = stream.tile(shape, F32, bufs=2)
+            nc.gpsimd.tensor_tensor(
                 out=gains[:],
                 in0=row_sb[:, rows, :].unsqueeze(3).to_broadcast(shape),
                 in1=col_sb[:, rows, :].unsqueeze(2).to_broadcast(shape),
                 op=MULT,
             )
-            gains_tiles[c] = gains
+            gains_tiles[v] = gains
 
         def stage_2(v):
             c, pair = divmod(v, 2)
-            if v == B // (2 * P) - 1:
-                s2_bank = psum_s1.tile([P, 2, OI], F32, name="s1_bank")
+            if v % 2 == 1 and PAIRS - 8 < v:
+                s2_bank = psum_hk.tile([P, 2, OI], F32, name="hk_bank")
             else:
                 s2_bank = psum_s2.tile([P, 2, OI], F32)
             for jj in range(2):
@@ -340,34 +351,29 @@ def tile_structuredternaryfactorgenerator_pa_t_kernel(
             s2_banks[v] = s2_bank
 
         def add_base(v):
-            c, pair = divmod(v, 2)
-            if pair == 0:
-                summed_tiles[c] = stream.tile([P, CHUNK_TILES, OI], F32, name="summed")
+            summed = stream.tile([P, 2, OI], F32, bufs=3)
             nc.vector.tensor_tensor(
-                out=summed_tiles[c][:, 2 * pair : 2 * pair + 2, :],
+                out=summed[:],
                 in0=s2_banks[v][:],
                 in1=base_all[:].unsqueeze(1).to_broadcast([P, 2, OI]),
                 op=ADD,
             )
+            summed_tiles[v] = summed
 
-        def scale_weight(c, tiles):
-            if tiles.start == 0:
-                weight_sb_tiles[c] = stream.tile([P, CHUNK_TILES, OI], F32, name="weight_sb")
-            weight_sb = weight_sb_tiles[c]
+        def scale_weight(v):
+            weight_sb = stream.tile([P, 2, OI], F32, bufs=3)
             nc.vector.tensor_tensor(
-                out=weight_sb[:, tiles, :],
-                in0=summed_tiles[c][:, tiles, :],
-                in1=gains_tiles[c][:, tiles, :, :].rearrange("p j o i -> p j (o i)"),
+                out=weight_sb[:],
+                in0=summed_tiles[v][:],
+                in1=gains_tiles[v][:].rearrange("p j o i -> p j (o i)"),
                 op=MULT,
             )
-            nc.sync.dma_start(
-                out=weight_rows[
-                    :, c * CHUNK_TILES + tiles.start : c * CHUNK_TILES + tiles.stop, :
-                ],
-                in_=weight_sb[:, tiles, :],
-            )
+            nc.sync.dma_start(out=weight_rows[:, 2 * v : 2 * v + 2, :], in_=weight_sb[:])
+            if v + 2 < PAIRS:
+                compute_gains(v + 2)
 
-        GAINS_STEP = {3: 0, 5: 1, 7: 2, 9: 3, 11: 4, 12: 5, 13: 6}
+        LATE = 2
+        CO_LAG = 3
         ALL = slice(0, CHUNK)
         LOW = slice(0, CHUNK // 2)
         HIGH = slice(CHUNK // 2, CHUNK)
@@ -379,114 +385,127 @@ def tile_structuredternaryfactorgenerator_pa_t_kernel(
                 transpose_coeff(s, j)
                 empty_coeff(s, j, copy_out)
 
+        def co_half(k):
+            coeff_out(k // 2, (2 * (k % 2), 2 * (k % 2) + 1), (copy_s, copy_s))
+
+        STAGE_2_MIDDLE = {STEPS - 2: STEPS - 5, STEPS - 1: STEPS - 3}
+        STAGE_2_END = {s: s - STAGE_2_LAG for s in range(STAGE_2_LAG, STEPS - 2)}
+        STAGE_2_END[STEPS - 2] = STEPS - 4
+
         def step(s):
-            even = s % 2 == 0
-            units = {1: [3, 4], 2: [5]}.get(s, [s + 3] if s + 3 < HK_UNITS else [])
-            v = s - 3
-            if even and s // 2 + 3 < CHUNKS:
-                load_hk(s // 2 + 3)
-            if 2 < s and s + 2 < HK_UNITS:
-                quantise_hk(s + 2)
-            if s == STEPS - 1:
-                stage_2(v)
-                add_base(v)
+            unit = s + HK_AHEAD
+            before = STAGE_2_END.get(s - 1)
+            late = LATE < s
+            if s % 2 == 0 and s // 2 + 4 < CHUNKS:
+                load_hk(s // 2 + 4)
+            if s == 3:
+                load_gains()
+                compute_gains(0)
+                compute_gains(1)
+            if before is not None and 0 < before:
+                scale_weight(before - 1)
+            if late and unit - 1 < HK_UNITS:
+                for pair in range(2):
+                    empty_hk(unit - 1, pair, copy_v)
+            if before is not None:
+                add_base(before)
+            if s == 2:
+                quantise_hk(4)
             for r in range(2):
-                if 2 <= s:
-                    coeff_out(s - 2, (2 * r, 2 * r + 1), (copy_s, copy_s))
-                if 2 <= s:
-                    for unit in units:
-                        transpose_hk(unit, r)
                 for t in (2 * r, 2 * r + 1):
                     stage_1(s, t)
                     tanh(s, t)
-                if s == 1:
-                    for pair in range(2):
-                        transpose_hk(units[r], pair)
-                        empty_hk(units[r], pair, (copy_s, copy_v)[pair])
-                    quantise_hk(units[r])
+                if r == 1 and s in STAGE_2_END:
+                    stage_2(STAGE_2_END[s])
+                if r == 0 and s in STAGE_2_MIDDLE:
+                    stage_2(STAGE_2_MIDDLE[s])
+                co_half(2 * s + r - CO_LAG)
+                if unit < HK_UNITS:
+                    transpose_hk(unit, r)
+                    if not late:
+                        empty_hk(unit, r, copy_s)
                 if r == 0:
-                    if 2 <= s:
-                        for unit in units:
-                            empty_hk(unit, 0, copy_v)
-                        regroup_coeff(s - 1, ALL)
-                    if s in GAINS_STEP:
-                        compute_gains(GAINS_STEP[s])
-                    if 0 <= v < STEPS - 4:
-                        stage_2(v)
-                        add_base(v)
-                    if s == STEPS - 1:
-                        stage_2(v + 1)
-                        quantise_coeff(s - 1, ALL)
-                        add_base(v + 1)
-                if r == 1:
-                    if 2 <= s:
-                        for unit in units:
-                            empty_hk(unit, 1, copy_v if even else copy_s)
-                    if s == 1:
-                        regroup_coeff(0, ALL)
+                    regroup_coeff(s - 1, ALL)
+                    if 2 < s and unit - 1 < HK_UNITS:
+                        quantise_hk(unit - 1)
+                    if s in STAGE_2_MIDDLE:
+                        scale_weight(STAGE_2_MIDDLE[s] - 1)
+                    quantise_coeff(s - 1, ALL)
+                    if s == 2:
                         regroup_bases()
-                    if s < STEPS - 1:
-                        quantise_coeff(s - 1, ALL)
-                    if s == 1:
                         quantise_bases()
-                    if 0 < v and (even or s == STEPS - 1):
-                        scale_weight(v // 2, slice(0, CHUNK_TILES))
-                    if s == STEPS - 2:
-                        compute_gains(CHUNKS - 1)
+                    if s in STAGE_2_MIDDLE:
+                        add_base(STAGE_2_MIDDLE[s])
+                elif s == 2:
+                    spread_base()
 
-        def first_step():
-            regroup_kw(0, 0, ALL, copy_v)
-            quantise_kw(0, 0)
+        def start():
+            regroup_kw(0, 0, LOW, copy_v)
+            regroup_kw(0, 0, HIGH, copy_s)
             for pair in range(2):
-                for unit in range(2):
-                    transpose_hk(unit, pair)
-                    empty_hk(unit, pair, (copy_s, copy_v)[unit])
-            keep_clock(2)
-            regroup_kw(0, 1, LOW, copy_v)
-            regroup_kw(0, 1, HIGH, copy_s)
+                transpose_hk(0, pair)
+                empty_hk(0, pair, copy_s)
+            keep_clock(3)
             prepare_bias()
-            spread_base()
+            quantise_kw(0, 0)
+            regroup_kw(0, 1, ALL, copy_v)
             quantise_hk(0)
-            quantise_hk(1)
+            for pair in range(2):
+                transpose_hk(1, pair)
+                empty_hk(1, pair, copy_s)
             quantise_kw(0, 1)
-            for t in range(3):
+            for t in range(4):
                 stage_1(0, t, (0,))
-            regroup_kw(1, 1, HIGH, copy_s)
             regroup_kw(1, 0, ALL, copy_v)
-            regroup_kw(1, 1, LOW, copy_v)
-            for t in range(3):
+            quantise_hk(1)
+            regroup_kw(1, 1, HIGH, copy_s)
+            for t in range(4):
                 stage_1(0, t, (1,))
                 tanh(0, t)
-            stage_1(0, 3)
-            tanh(0, 3)
             quantise_kw(1, 0)
+            regroup_kw(1, 1, LOW, copy_v)
             quantise_kw(1, 1)
             for pair in range(2):
                 transpose_hk(2, pair)
-                empty_hk(2, pair, copy_s)
+                empty_hk(2, pair, copy_v)
+            for t in range(4):
+                stage_1(1, t, (0,))
+            for pair in range(2):
+                transpose_hk(3, pair)
+                empty_hk(3, pair, (copy_s, copy_v)[pair])
             quantise_hk(2)
-            load_hk(3)
+            for t in range(4):
+                stage_1(1, t, (1,))
+                tanh(1, t)
+            quantise_hk(3)
+            for pair in range(2):
+                transpose_hk(4, pair)
+                empty_hk(4, pair, copy_v)
+            regroup_coeff(0, ALL)
+            quantise_coeff(0, ALL)
+            co_half(0)
+            load_hk(4)
 
         def tail():
             last = STEPS - 1
             v = STEPS - 2
-            coeff_out(last - 1, (0, 1), (copy_s, copy_s))
             keep_clock(3)
-            coeff_out(last - 1, (2, 3), (copy_s, copy_s))
+            co_half(2 * last - 1)
             regroup_coeff(last, LOW)
             regroup_coeff(last, HIGH)
             quantise_coeff(last, LOW)
             quantise_coeff(last, HIGH)
+            scale_weight(v - 1)
             stage_2(v)
             coeff_out(last, (0, 1), (copy_s, copy_s))
             stage_2(v + 1)
             coeff_out(last, (2, 3), (copy_s, copy_s))
             add_base(v)
-            scale_weight(CHUNKS - 1, slice(0, 2))
             add_base(v + 1)
-            scale_weight(CHUNKS - 1, slice(2, 4))
+            scale_weight(v)
+            scale_weight(v + 1)
 
-        first_step()
-        for s in range(1, STEPS):
+        start()
+        for s in range(2, STEPS):
             step(s)
         tail()

@@ -25,7 +25,6 @@ I = 16
 OI = O * I
 H_PASSES = H // K_PASS
 K_PASSES = K // K_PASS
-ROWS_PER_PARTITION = B // P
 CHUNK_TILES = 4
 CHUNK = CHUNK_TILES * P
 CHUNKS = B // CHUNK
@@ -43,9 +42,9 @@ def tile_structuredternaryfactorgenerator_pa_t_kernel(
 ):
     nc = tc.nc
 
-    hk_rows = hk.rearrange("(p j) h -> p j h", j=ROWS_PER_PARTITION)
-    coeff_rows = out_1.rearrange("(p j) k -> p j k", j=ROWS_PER_PARTITION)
-    weight_rows = out_0.rearrange("(p j) o i -> p j (o i)", j=ROWS_PER_PARTITION)
+    hk_rows = hk.rearrange("(p c j) h -> c p j h", j=CHUNK_TILES, c=CHUNKS)
+    coeff_rows = out_1.rearrange("(p c j) k -> c p j k", j=CHUNK_TILES, c=CHUNKS)
+    weight_rows = out_0.rearrange("(p c j) o i -> c p j (o i)", j=CHUNK_TILES, c=CHUNKS)
 
     with ExitStack() as stack:
         const = stack.enter_context(tc.tile_pool(name="const", bufs=1))
@@ -71,22 +70,20 @@ def tile_structuredternaryfactorgenerator_pa_t_kernel(
         gains_tiles = {}
         summed_tiles = {}
 
-        def load_hk(c, features=slice(0, H)):
+        def load_hk(c, tiles=slice(0, CHUNK_TILES)):
             if c not in hk_tiles:
                 hk_tiles[c] = stream.tile([P, CHUNK_TILES, H], BF16, name="hk_sb", bufs=4)
-            first = c * CHUNK_TILES
-            nc.sync.dma_start(
-                out=hk_tiles[c][:, :, features],
-                in_=hk_rows[:, first : first + CHUNK_TILES, features],
-            )
+            nc.sync.dma_start(out=hk_tiles[c][:, tiles, :], in_=hk_rows[c, :, tiles, :])
+
+        row_sb = const.tile([P, CHUNKS, CHUNK_TILES, O], BF16)
+        col_sb = const.tile([P, CHUNKS, CHUNK_TILES, I], BF16)
 
         def load_gains():
-            nc.sync.dma_start(
-                out=row_sb[:], in_=row.rearrange("(p j) o -> p j o", j=ROWS_PER_PARTITION)
-            )
-            nc.sync.dma_start(
-                out=col_sb[:], in_=col.rearrange("(p j) i -> p j i", j=ROWS_PER_PARTITION)
-            )
+            for gain_sb, gain in ((row_sb, row), (col_sb, col)):
+                nc.sync.dma_start(
+                    out=gain_sb[:],
+                    in_=gain.rearrange("(p c j) o -> p c j o", j=CHUNK_TILES, c=CHUNKS),
+                )
 
         kw_raw = setup.tile([P, K_PASSES, H_PASSES * PACK, K_PASS], BF16)
         kw_view = kw2.rearrange("(a w e) k -> w a e k", w=P, e=2)
@@ -106,22 +103,21 @@ def tile_structuredternaryfactorgenerator_pa_t_kernel(
         nc.vector.memset(kb_rows[:], 0.0)
         base_row = setup.tile([P, OI], BF16)
         nc.vector.memset(base_row[:], 0.0)
-        row_sb = const.tile([P, ROWS_PER_PARTITION, O], BF16)
-        col_sb = const.tile([P, ROWS_PER_PARTITION, I], BF16)
         bases_raw = setup.tile([P, K_PASSES * PACK, OI], BF16)
 
-        first_half = slice(0, K_PASS)
-        second_half = slice(K_PASS, H)
+        first_tiles = slice(0, 2)
+        last_tiles = slice(2, 4)
         load_kw(0, (0, 1))
-        load_hk(0, first_half)
+        load_hk(0, first_tiles)
+        load_hk(0, last_tiles)
         nc.sync.dma_start(out=kb_rows[0 : K // P, :], in_=kb2.rearrange("(m p) -> m p", p=P))
-        load_kw(0, (2, 3))
-        load_hk(0, second_half)
-        load_kw(1, range(4))
-        load_hk(1, first_half)
-        load_hk(1, second_half)
         nc.sync.dma_start(out=base_row[0:1, :], in_=base.rearrange("(a o) i -> a (o i)", a=1))
+        load_kw(0, (2, 3))
+        load_kw(1, range(4))
+        load_hk(1, first_tiles)
+        load_hk(1, last_tiles)
         load_hk(2)
+        load_gains()
         nc.sync.dma_start(out=bases_raw[:], in_=bases.rearrange("(a p) o i -> p a (o i)", p=P))
         load_hk(3)
 
@@ -129,11 +125,20 @@ def tile_structuredternaryfactorgenerator_pa_t_kernel(
         make_identity(nc, ident[:])
 
         def keep_clock(n):
-            s1_bank = psum_s1.tile([P, BANK], F32)
+            s2_bank = psum_s2.tile([P, BANK], F32)
             for i in range(n):
-                nc.tensor.matmul(s1_bank[:], lhsT=ones[:], rhs=zeros[:], start=True, stop=True)
+                nc.tensor.matmul(s2_bank[:], lhsT=ones[:], rhs=zeros[:], start=True, stop=True)
 
-        keep_clock(9)
+        keep_clock(5)
+
+        def multiply_gains(multiply, gains, rows, cols):
+            shape = [P, 2, O, I]
+            multiply(
+                out=gains[:],
+                in0=rows.unsqueeze(3).to_broadcast(shape),
+                in1=cols.unsqueeze(2).to_broadcast(shape),
+                op=MULT,
+            )
 
         kb = const.tile([P, K // P], F32)
 
@@ -155,11 +160,12 @@ def tile_structuredternaryfactorgenerator_pa_t_kernel(
 
         kw_grouped_tiles = {}
 
-        def regroup_kw(G, g, cols, copy_out):
+        def regroup_kw(G, g, quads, copy_out):
             if (G, g) not in kw_grouped_tiles:
                 kw_grouped_tiles[G, g] = setup.tile(
                     [P, K_PASS, PACK], BF16, name="kw_grouped", align_bytes=64, bufs=4
                 )
+            cols = slice(quads[0] * P, (quads[-1] + 1) * P)
             copy_out(
                 out=kw_grouped_tiles[G, g][:, cols, :].rearrange("p (c i) t -> p c t i", i=4),
                 in_=kw_raw[:, G, g * PACK : (g + 1) * PACK, cols].rearrange(
@@ -180,7 +186,6 @@ def tile_structuredternaryfactorgenerator_pa_t_kernel(
                 base_bank[:, 0:OI], lhsT=ones[:], rhs=base_row[:], start=True, stop=True
             )
             nc.scalar.copy(out=base_all[:], in_=base_bank[:, 0:OI])
-
 
         bases_grouped = setup.tile([P, K_PASSES, OI, PACK], BF16, align_bytes=64)
 
@@ -204,7 +209,7 @@ def tile_structuredternaryfactorgenerator_pa_t_kernel(
             c, g = divmod(unit, H_PASSES)
             hk_words = hk_tiles[c][:].rearrange("p j h -> p (j h)").bitcast(F32)
             words_per_row = H // 2
-            if unit == 1:
+            if (unit < 2 and unit % 2 == 1) or (unit in (2, 3) and pair == 1):
                 hk_bank = psum_co.tile([P, BANK], F32, name="co_bank")
             else:
                 hk_bank = psum_hk.tile([P, BANK], F32)
@@ -219,7 +224,7 @@ def tile_structuredternaryfactorgenerator_pa_t_kernel(
             hk_banks[unit, pair] = hk_bank
 
         def empty_hk(unit, pair, copy_out):
-            if pair == 0:
+            if unit not in hk_grouped_tiles:
                 hk_grouped_tiles[unit] = stream.tile(
                     [P, CHUNK * PACK], BF16, name="hk_grouped", align_bytes=64, bufs=4
                 )
@@ -239,54 +244,55 @@ def tile_structuredternaryfactorgenerator_pa_t_kernel(
             )
             hk_quantised[unit] = (hk_codes, hk_scales)
 
-        def stage_1(s, t, passes=range(H_PASSES), cols=slice(0, CHUNK)):
+        def stage_1(s, t, passes=range(H_PASSES)):
             c, G = divmod(s, K_PASSES)
             if passes[0] == 0:
-                if s == 0 and t == PACK - 1:
-                    s1_banks[s, t] = psum_co.tile([P, BANK], F32, name="co_bank")
-                elif s == 1 and t == PACK - 1:
+                if s < 2 and t == PACK - 1:
                     s1_banks[s, t] = psum_s2.tile([P, BANK], F32, name="s2_bank")
                 else:
                     s1_banks[s, t] = psum_s1.tile([P, BANK], F32, name="s1_bank")
             for g in passes:
                 hk_codes, hk_scales = hk_quantised[c * H_PASSES + g]
                 nc.tensor.matmul_mx(
-                    out=s1_banks[s, t][:, cols],
+                    out=s1_banks[s, t][:],
                     lhsT=kw_codes[:, G, g, t * P : (t + 1) * P].bitcast(FP8X4),
                     lhsT_scale=kw_scales[:, G, g, t * P : (t + 1) * P],
-                    rhs=hk_codes[:, cols].bitcast(FP8X4),
-                    rhs_scale=hk_scales[:, cols],
+                    rhs=hk_codes[:].bitcast(FP8X4),
+                    rhs_scale=hk_scales[:],
                     start=(g == 0),
                     stop=(g == H_PASSES - 1),
                 )
 
-        def tanh(s, t, cols=slice(0, CHUNK)):
-            if t == 0 and cols.start == 0:
+        def tanh(s, t):
+            if t == 0:
                 coeff_t_tiles[s] = stream.tile([P, PACK, CHUNK], F32, name="coeff_t", bufs=4)
             m = s % K_PASSES * PACK + t
             nc.scalar.activation(
-                out=coeff_t_tiles[s][:, t, cols],
-                in_=s1_banks[s, t][:, cols],
+                out=coeff_t_tiles[s][:, t, :],
+                in_=s1_banks[s, t][:],
                 func=TANH,
                 bias=kb[:, m : m + 1],
             )
 
-        def regroup_coeff(s, cols):
-            if cols.start == 0:
+        def regroup_coeff(s, tiles=range(CHUNK_TILES)):
+            if tiles[0] == 0:
                 coeff_grouped_tiles[s] = stream.tile(
                     [P, CHUNK, PACK], BF16, name="coeff_grouped", align_bytes=64
                 )
+            a, b = tiles[0], tiles[-1] + 1
+            grouped = coeff_grouped_tiles[s][:, a * P : b * P, :]
             nc.vector.tensor_copy(
-                out=coeff_grouped_tiles[s][:, cols, :].rearrange("p (c i) t -> p c t i", i=4),
-                in_=coeff_t_tiles[s][:, :, cols].rearrange("p t (c i) -> p c t i", i=4),
+                out=grouped.rearrange("p (c i) t -> p c t i", i=4),
+                in_=coeff_t_tiles[s][:, :, a * P : b * P].rearrange("p t (c i) -> p c t i", i=4),
             )
 
-        def quantise_coeff(s, cols):
-            if cols.start == 0:
-                coeff_codes = stream.tile([P, CHUNK], U32, align_bytes=64, bufs=6)
-                coeff_scales = stream.tile([P, CHUNK], U8, align_bytes=64, bufs=6)
+        def quantise_coeff(s, tiles=range(CHUNK_TILES)):
+            if tiles[0] == 0:
+                coeff_codes = stream.tile([P, CHUNK], U32, align_bytes=64, bufs=8)
+                coeff_scales = stream.tile([P, CHUNK], U8, align_bytes=64, bufs=8)
                 coeff_quantised[s] = (coeff_codes, coeff_scales)
             coeff_codes, coeff_scales = coeff_quantised[s]
+            cols = slice(tiles[0] * P, (tiles[-1] + 1) * P)
             nc.vector.quantize_mx(
                 out=coeff_codes[:, cols].bitcast(FP8X4),
                 scales=coeff_scales[:, cols],
@@ -294,7 +300,12 @@ def tile_structuredternaryfactorgenerator_pa_t_kernel(
             )
 
         def transpose_coeff(s, j):
-            co_bank = psum_co.tile([P, BANK], F32)
+            if s == STEPS - 1 and j < 2:
+                co_bank = psum_s1.tile([P, BANK], F32, name="s1_bank")
+            elif s == STEPS - 2 and j >= 2:
+                co_bank = psum_hk.tile([P, BANK], F32, name="hk_bank")
+            else:
+                co_bank = psum_co.tile([P, BANK], F32)
             for t in range(PACK):
                 nc.tensor.transpose(
                     co_bank[:, t * P : (t + 1) * P],
@@ -306,33 +317,31 @@ def tile_structuredternaryfactorgenerator_pa_t_kernel(
         def empty_coeff(s, j, copy_out):
             c, G = divmod(s, K_PASSES)
             if j % 2 == 0:
-                coeff_sb_tiles[s, j // 2] = stream.tile(
-                    [P, 2, BANK], F32, name="coeff_sb", bufs=6
-                )
+                coeff_sb_tiles[s, j // 2] = stream.tile([P, 2, BANK], F32, name="coeff_sb", bufs=4)
             coeff_sb = coeff_sb_tiles[s, j // 2]
             copy_out(out=coeff_sb[:, j % 2, :], in_=co_banks[s, j][:])
-            if j % 2 == 1:
-                first = c * CHUNK_TILES + j - 1
+            if s >= STEPS - 2:
                 nc.sync.dma_start(
-                    out=coeff_rows[:, first : first + 2, G * BANK : (G + 1) * BANK], in_=coeff_sb[:]
+                    out=coeff_rows[c, :, j, G * BANK : (G + 1) * BANK], in_=coeff_sb[:, j % 2, :]
+                )
+            elif j % 2 == 1:
+                nc.sync.dma_start(
+                    out=coeff_rows[c, :, j - 1 : j + 1, G * BANK : (G + 1) * BANK], in_=coeff_sb[:]
                 )
 
         def compute_gains(v):
-            rows = slice(2 * v, 2 * v + 2)
-            shape = [P, 2, O, I]
-            gains = stream.tile(shape, F32, bufs=2)
-            nc.gpsimd.tensor_tensor(
-                out=gains[:],
-                in0=row_sb[:, rows, :].unsqueeze(3).to_broadcast(shape),
-                in1=col_sb[:, rows, :].unsqueeze(2).to_broadcast(shape),
-                op=MULT,
+            c, pair = divmod(v, 2)
+            tiles = slice(2 * pair, 2 * pair + 2)
+            gains = stream.tile([P, 2, O, I], F32, bufs=10)
+            multiply_gains(
+                nc.vector.tensor_tensor, gains, row_sb[:, c, tiles, :], col_sb[:, c, tiles, :]
             )
             gains_tiles[v] = gains
 
         def stage_2(v):
             c, pair = divmod(v, 2)
-            if v % 2 == 1 and PAIRS - 8 < v:
-                s2_bank = psum_hk.tile([P, 2, OI], F32, name="hk_bank")
+            if v == PAIRS - 1 or v % 2 == 1 and PAIRS - 6 < v:
+                s2_bank = psum_s1.tile([P, 2, OI], F32, name="s1_bank")
             else:
                 s2_bank = psum_s2.tile([P, 2, OI], F32)
             for jj in range(2):
@@ -361,6 +370,7 @@ def tile_structuredternaryfactorgenerator_pa_t_kernel(
             summed_tiles[v] = summed
 
         def scale_weight(v):
+            c, pair = divmod(v, 2)
             weight_sb = stream.tile([P, 2, OI], F32, bufs=3)
             nc.vector.tensor_tensor(
                 out=weight_sb[:],
@@ -368,141 +378,127 @@ def tile_structuredternaryfactorgenerator_pa_t_kernel(
                 in1=gains_tiles[v][:].rearrange("p j o i -> p j (o i)"),
                 op=MULT,
             )
-            nc.sync.dma_start(out=weight_rows[:, 2 * v : 2 * v + 2, :], in_=weight_sb[:])
-            if v + 2 < PAIRS:
-                compute_gains(v + 2)
+            nc.sync.dma_start(out=weight_rows[c, :, 2 * pair : 2 * pair + 2, :], in_=weight_sb[:])
 
-        LATE = 2
+        GS = 4
         CO_LAG = 3
-        ALL = slice(0, CHUNK)
-        LOW = slice(0, CHUNK // 2)
-        HIGH = slice(CHUNK // 2, CHUNK)
+        LOW = range(0, 2)
+        HIGH = range(2, 4)
+        ALL = range(4)
         copy_v = nc.vector.tensor_copy
         copy_s = nc.scalar.copy
 
-        def coeff_out(s, tiles, copies):
-            for j, copy_out in zip(tiles, copies):
-                transpose_coeff(s, j)
-                empty_coeff(s, j, copy_out)
+        def co_half(k, copies=None):
+            if 0 <= k < 2 * STEPS:
+                for i, j in enumerate((2 * (k % 2), 2 * (k % 2) + 1)):
+                    transpose_coeff(k // 2, j)
+                    empty_coeff(k // 2, j, copies[i] if copies else copy_s)
 
-        def co_half(k):
-            coeff_out(k // 2, (2 * (k % 2), 2 * (k % 2) + 1), (copy_s, copy_s))
-
-        STAGE_2_MIDDLE = {STEPS - 2: STEPS - 5, STEPS - 1: STEPS - 3}
-        STAGE_2_END = {s: s - STAGE_2_LAG for s in range(STAGE_2_LAG, STEPS - 2)}
-        STAGE_2_END[STEPS - 2] = STEPS - 4
+        MIDDLE = {STEPS - 2: STEPS - 5, STEPS - 1: STEPS - 3}
+        END = {s: s - STAGE_2_LAG for s in range(STAGE_2_LAG, STEPS - 2)}
+        END[STEPS - 2] = STEPS - 4
 
         def step(s):
-            unit = s + HK_AHEAD
-            before = STAGE_2_END.get(s - 1)
-            late = LATE < s
+            before = END.get(s - 1)
+            middle = MIDDLE.get(s)
+            unit = s + 3
             if s % 2 == 0 and s // 2 + 4 < CHUNKS:
                 load_hk(s // 2 + 4)
-            if s == 3:
-                load_gains()
-                compute_gains(0)
-                compute_gains(1)
-            if before is not None and 0 < before:
+            if before:
                 scale_weight(before - 1)
-            if late and unit - 1 < HK_UNITS:
-                for pair in range(2):
-                    empty_hk(unit - 1, pair, copy_v)
+            if 3 < s and unit - 1 < HK_UNITS:
+                empty_hk(unit - 1, 0, copy_v)
             if before is not None:
                 add_base(before)
-            if s == 2:
-                quantise_hk(4)
             for r in range(2):
                 for t in (2 * r, 2 * r + 1):
                     stage_1(s, t)
                     tanh(s, t)
-                if r == 1 and s in STAGE_2_END:
-                    stage_2(STAGE_2_END[s])
-                if r == 0 and s in STAGE_2_MIDDLE:
-                    stage_2(STAGE_2_MIDDLE[s])
+                if r == 0 and middle is not None:
+                    stage_2(middle)
+                if r == 1 and s in END:
+                    stage_2(END[s])
                 co_half(2 * s + r - CO_LAG)
-                if unit < HK_UNITS:
+                if s == 2:
+                    for pair in range(2):
+                        transpose_hk(4 + r, pair)
+                        empty_hk(4 + r, pair, (copy_v, copy_s)[r])
+                    quantise_hk(4 + r)
+                elif unit < HK_UNITS:
                     transpose_hk(unit, r)
-                    if not late:
+                    if r == 1:
                         empty_hk(unit, r, copy_s)
                 if r == 0:
-                    regroup_coeff(s - 1, ALL)
-                    if 2 < s and unit - 1 < HK_UNITS:
+                    regroup_coeff(s - 1)
+                    if 3 < s and unit - 1 < HK_UNITS:
                         quantise_hk(unit - 1)
-                    if s in STAGE_2_MIDDLE:
-                        scale_weight(STAGE_2_MIDDLE[s] - 1)
-                    quantise_coeff(s - 1, ALL)
-                    if s == 2:
-                        regroup_bases()
-                        quantise_bases()
-                    if s in STAGE_2_MIDDLE:
-                        add_base(STAGE_2_MIDDLE[s])
-                elif s == 2:
-                    spread_base()
+                    if middle is not None:
+                        scale_weight(middle - 1)
+                    quantise_coeff(s - 1)
+                    for w in range(2 * s - 2 * GS, 2 * s - 2 * GS + 2):
+                        if 0 <= w < PAIRS:
+                            compute_gains(w)
+                    if middle is not None:
+                        add_base(middle)
+                if s == 2 and r == 0:
+                    regroup_bases()
+                    quantise_bases()
 
         def start():
-            regroup_kw(0, 0, LOW, copy_v)
-            regroup_kw(0, 0, HIGH, copy_s)
-            for pair in range(2):
-                transpose_hk(0, pair)
-                empty_hk(0, pair, copy_s)
-            keep_clock(3)
-            prepare_bias()
+            regroup_kw(0, 0, ALL, copy_v)
             quantise_kw(0, 0)
-            regroup_kw(0, 1, ALL, copy_v)
-            quantise_hk(0)
             for pair in range(2):
-                transpose_hk(1, pair)
-                empty_hk(1, pair, copy_s)
+                for unit in range(2):
+                    transpose_hk(unit, pair)
+                    empty_hk(unit, pair, copy_v if pair < unit else copy_s)
+            keep_clock(3)
+            regroup_kw(0, 1, ALL, copy_v)
+            prepare_bias()
+            spread_base()
+            quantise_hk(0)
+            quantise_hk(1)
             quantise_kw(0, 1)
             for t in range(4):
                 stage_1(0, t, (0,))
-            regroup_kw(1, 0, ALL, copy_v)
-            quantise_hk(1)
             regroup_kw(1, 1, HIGH, copy_s)
+            regroup_kw(1, 0, ALL, copy_v)
+            regroup_kw(1, 1, LOW, copy_v)
             for t in range(4):
                 stage_1(0, t, (1,))
                 tanh(0, t)
             quantise_kw(1, 0)
-            regroup_kw(1, 1, LOW, copy_v)
             quantise_kw(1, 1)
             for pair in range(2):
-                transpose_hk(2, pair)
-                empty_hk(2, pair, copy_v)
+                for unit in (2, 3):
+                    transpose_hk(unit, pair)
+                    empty_hk(unit, pair, (copy_s, copy_v)[pair])
             for t in range(4):
-                stage_1(1, t, (0,))
-            for pair in range(2):
-                transpose_hk(3, pair)
-                empty_hk(3, pair, (copy_s, copy_v)[pair])
-            quantise_hk(2)
-            for t in range(4):
-                stage_1(1, t, (1,))
+                stage_1(1, t)
                 tanh(1, t)
+            quantise_hk(2)
             quantise_hk(3)
-            for pair in range(2):
-                transpose_hk(4, pair)
-                empty_hk(4, pair, copy_v)
-            regroup_coeff(0, ALL)
-            quantise_coeff(0, ALL)
-            co_half(0)
+            co_half(0, (copy_v, copy_v))
+            regroup_coeff(0)
+            quantise_coeff(0)
             load_hk(4)
 
         def tail():
             last = STEPS - 1
             v = STEPS - 2
-            keep_clock(3)
             co_half(2 * last - 1)
             regroup_coeff(last, LOW)
             regroup_coeff(last, HIGH)
             quantise_coeff(last, LOW)
             quantise_coeff(last, HIGH)
             scale_weight(v - 1)
+            keep_clock(3)
+            co_half(2 * last, (copy_v, copy_s))
             stage_2(v)
-            coeff_out(last, (0, 1), (copy_s, copy_s))
+            co_half(2 * last + 1)
             stage_2(v + 1)
-            coeff_out(last, (2, 3), (copy_s, copy_s))
             add_base(v)
-            add_base(v + 1)
             scale_weight(v)
+            add_base(v + 1)
             scale_weight(v + 1)
 
         start()

@@ -32,6 +32,7 @@ PAIRS = B // (2 * P)
 STEPS = CHUNKS * K_PASSES
 HK_UNITS = CHUNKS * H_PASSES
 HK_AHEAD = 3
+GAINS_BUFS = 3
 STAGE_2_LAG = 3
 
 FLOPS = 2 * B * H * K + 2 * B * K * OI
@@ -329,12 +330,12 @@ def tile_structuredternaryfactorgenerator_pa_t_kernel(
                     out=coeff_rows[c, :, j - 1 : j + 1, G * BANK : (G + 1) * BANK], in_=coeff_sb[:]
                 )
 
-        def compute_gains(v):
+        def compute_gains(v, multiply):
             c, pair = divmod(v, 2)
             tiles = slice(2 * pair, 2 * pair + 2)
-            gains = stream.tile([P, 2, O, I], F32, bufs=10)
+            gains = stream.tile([P, 2, O, I], F32, bufs=GAINS_BUFS)
             multiply_gains(
-                nc.vector.tensor_tensor, gains, row_sb[:, c, tiles, :], col_sb[:, c, tiles, :]
+                multiply, gains, row_sb[:, c, tiles, :], col_sb[:, c, tiles, :]
             )
             gains_tiles[v] = gains
 
@@ -379,9 +380,12 @@ def tile_structuredternaryfactorgenerator_pa_t_kernel(
                 op=MULT,
             )
             nc.sync.dma_start(out=weight_rows[c, :, 2 * pair : 2 * pair + 2, :], in_=weight_sb[:])
+            if v + GAINS_BUFS < PAIRS:
+                compute_gains(v + GAINS_BUFS, nc.gpsimd.tensor_tensor)
 
         GS = 4
         CO_LAG = 3
+        BOTH = range(5, HK_UNITS - 4)
         LOW = range(0, 2)
         HIGH = range(2, 4)
         ALL = range(4)
@@ -408,6 +412,8 @@ def tile_structuredternaryfactorgenerator_pa_t_kernel(
                 scale_weight(before - 1)
             if 3 < s and unit - 1 < HK_UNITS:
                 empty_hk(unit - 1, 0, copy_v)
+                if s - 1 in BOTH:
+                    empty_hk(unit - 1, 1, copy_v)
             if before is not None:
                 add_base(before)
             for r in range(2):
@@ -426,7 +432,7 @@ def tile_structuredternaryfactorgenerator_pa_t_kernel(
                     quantise_hk(4 + r)
                 elif unit < HK_UNITS:
                     transpose_hk(unit, r)
-                    if r == 1:
+                    if r == 1 and s not in BOTH:
                         empty_hk(unit, r, copy_s)
                 if r == 0:
                     regroup_coeff(s - 1)
@@ -436,8 +442,8 @@ def tile_structuredternaryfactorgenerator_pa_t_kernel(
                         scale_weight(middle - 1)
                     quantise_coeff(s - 1)
                     for w in range(2 * s - 2 * GS, 2 * s - 2 * GS + 2):
-                        if 0 <= w < PAIRS:
-                            compute_gains(w)
+                        if 0 <= w < GAINS_BUFS:
+                            compute_gains(w, nc.vector.tensor_tensor)
                     if middle is not None:
                         add_base(middle)
                 if s == 2 and r == 0:

@@ -130,7 +130,7 @@ def tile_structuredternaryfactorgenerator_pa_t_kernel(
             for i in range(n):
                 nc.tensor.matmul(s2_bank[:], lhsT=ones[:], rhs=zeros[:], start=True, stop=True)
 
-        keep_clock(5)
+        keep_clock(7)
 
         def multiply_gains(multiply, gains, rows, cols):
             shape = [P, 2, O, I]
@@ -420,6 +420,8 @@ def tile_structuredternaryfactorgenerator_pa_t_kernel(
                 for t in (2 * r, 2 * r + 1):
                     stage_1(s, t)
                     tanh(s, t)
+                if s == 2 and r == 1:
+                    keep_clock(1)
                 if r == 0 and middle is not None:
                     stage_2(middle)
                 if r == 1 and s in END:
@@ -456,9 +458,10 @@ def tile_structuredternaryfactorgenerator_pa_t_kernel(
             for pair in range(2):
                 for unit in range(2):
                     transpose_hk(unit, pair)
-                    empty_hk(unit, pair, copy_v if pair < unit else copy_s)
+                    empty_hk(unit, pair, copy_s)
             keep_clock(3)
-            regroup_kw(0, 1, ALL, copy_v)
+            regroup_kw(0, 1, range(0, 3), copy_v)
+            regroup_kw(0, 1, range(3, 4), copy_s)
             prepare_bias()
             spread_base()
             quantise_hk(0)
@@ -498,7 +501,7 @@ def tile_structuredternaryfactorgenerator_pa_t_kernel(
             quantise_coeff(last, HIGH)
             scale_weight(v - 1)
             keep_clock(3)
-            co_half(2 * last, (copy_v, copy_s))
+            co_half(2 * last, (copy_s, copy_v))
             stage_2(v)
             co_half(2 * last + 1)
             stage_2(v + 1)

from contextlib import ExitStack

import concourse.mybir as mybir
from concourse.masks import make_identity

F32 = mybir.dt.float32
BF16 = mybir.dt.bfloat16
U32 = mybir.dt.uint32
U8 = mybir.dt.uint8
FP8X4 = mybir.dt.float8_e4m3fn_x4
TANH = mybir.ActivationFunctionType.Tanh
ADD = mybir.AluOpType.add
MULT = mybir.AluOpType.mult

P = 128
PACK = 4
K_PASS = P * PACK
BANK = 512

B = 4096
H = 1024
K = 1024
O = 16
I = 16
OI = O * I
H_PASSES = H // K_PASS
K_PASSES = K // K_PASS
CHUNK_TILES = 4
CHUNK = CHUNK_TILES * P
CHUNKS = B // CHUNK
PAIRS = B // (2 * P)
STEPS = CHUNKS * K_PASSES
HK_UNITS = CHUNKS * H_PASSES
HK_AHEAD = 3
GAINS_BUFS = 3
STAGE_2_LAG = 3

FLOPS = 2 * B * H * K + 2 * B * K * OI


def tile_structuredternaryfactorgenerator_pa_t_kernel(
    tc, hk, kw2, kb2, bases, base, row, col, out_0, out_1
):
    nc = tc.nc

    hk_rows = hk.rearrange("(p c j) h -> c p j h", j=CHUNK_TILES, c=CHUNKS)
    coeff_rows = out_1.rearrange("(p c j) k -> c p j k", j=CHUNK_TILES, c=CHUNKS)
    weight_rows = out_0.rearrange("(p c j) o i -> c p j (o i)", j=CHUNK_TILES, c=CHUNKS)

    with ExitStack() as stack:
        const = stack.enter_context(tc.tile_pool(name="const", bufs=1))
        setup = stack.enter_context(tc.tile_pool(name="setup", bufs=1))
        stream = stack.enter_context(tc.tile_pool(name="stream", bufs=2))
        psum_hk = stack.enter_context(tc.psum_pool(name="psum_hk", bufs=2))
        psum_s1 = stack.enter_context(tc.psum_pool(name="psum_s1", bufs=3))
        psum_co = stack.enter_context(tc.psum_pool(name="psum_co", bufs=2))
        psum_s2 = stack.enter_context(tc.psum_pool(name="psum_s2", bufs=1))
        stack.enter_context(tc.manual_schedule())

        hk_tiles = {}
        hk_banks = {}
        co_banks = {}
        s1_banks = {}
        s2_banks = {}
        hk_grouped_tiles = {}
        hk_quantised = {}
        coeff_t_tiles = {}
        coeff_grouped_tiles = {}
        coeff_quantised = {}
        coeff_sb_tiles = {}
        gains_tiles = {}
        summed_tiles = {}

        def load_hk(c, tiles=slice(0, CHUNK_TILES)):
            if c not in hk_tiles:
                hk_tiles[c] = stream.tile([P, CHUNK_TILES, H], BF16, name="hk_sb", bufs=4)
            nc.sync.dma_start(out=hk_tiles[c][:, tiles, :], in_=hk_rows[c, :, tiles, :])

        row_sb = const.tile([P, CHUNKS, CHUNK_TILES, O], BF16)
        col_sb = const.tile([P, CHUNKS, CHUNK_TILES, I], BF16)

        def load_gains():
            for gain_sb, gain in ((row_sb, row), (col_sb, col)):
                nc.sync.dma_start(
                    out=gain_sb[:],
                    in_=gain.rearrange("(p c j) o -> p c j o", j=CHUNK_TILES, c=CHUNKS),
                )

        kw_raw = setup.tile([P, K_PASSES, H_PASSES * PACK, K_PASS], BF16)
        kw_view = kw2.rearrange("(a w e) k -> w a e k", w=P, e=2)

        def load_kw(G, blocks):
            for a in blocks:
                nc.sync.dma_start(
                    out=kw_raw[:, G, 2 * a : 2 * a + 2, :],
                    in_=kw_view[:, a, :, G * K_PASS : (G + 1) * K_PASS],
                )

        ones = const.tile([P, P], BF16)
        nc.vector.memset(ones[:], 1.0)
        zeros = const.tile([P, BANK], BF16)
        nc.gpsimd.memset(zeros[:], 0.0)
        kb_rows = setup.tile([P, P], BF16)
        nc.vector.memset(kb_rows[:], 0.0)
        base_row = setup.tile([P, OI], BF16)
        nc.vector.memset(base_row[:], 0.0)
        bases_raw = setup.tile([P, K_PASSES * PACK, OI], BF16)

        first_tiles = slice(0, 2)
        last_tiles = slice(2, 4)
        load_kw(0, (0, 1))
        load_hk(0, first_tiles)
        load_hk(0, last_tiles)
        nc.sync.dma_start(out=kb_rows[0 : K // P, :], in_=kb2.rearrange("(m p) -> m p", p=P))
        nc.sync.dma_start(out=base_row[0:1, :], in_=base.rearrange("(a o) i -> a (o i)", a=1))
        load_kw(0, (2, 3))
        load_kw(1, range(4))
        load_hk(1, first_tiles)
        load_hk(1, last_tiles)
        load_hk(2)
        load_gains()
        nc.sync.dma_start(out=bases_raw[:], in_=bases.rearrange("(a p) o i -> p a (o i)", p=P))
        load_hk(3)

        ident = const.tile([P, P], F32)
        make_identity(nc, ident[:])

        def keep_clock(n):
            s2_bank = psum_s2.tile([P, BANK], F32)
            for i in range(n):
                nc.tensor.matmul(s2_bank[:], lhsT=ones[:], rhs=zeros[:], start=True, stop=True)

        keep_clock(7)

        def multiply_gains(multiply, gains, rows, cols):
            shape = [P, 2, O, I]
            multiply(
                out=gains[:],
                in0=rows.unsqueeze(3).to_broadcast(shape),
                in1=cols.unsqueeze(2).to_broadcast(shape),
                op=MULT,
            )

        kb = const.tile([P, K // P], F32)

        def prepare_bias():
            kb_rows_f32 = setup.tile([P, P], F32)
            nc.scalar.copy(out=kb_rows_f32[:], in_=kb_rows[:])
            kb_bank = psum_co.tile([P, BANK], F32, name="co_bank")
            nc.tensor.transpose(kb_bank[:, 0:P], kb_rows_f32[:], ident[:])
            nc.scalar.copy(out=kb[:], in_=kb_bank[:, 0 : K // P])

        warm = setup.tile([P, 1], F32)
        nc.scalar.activation(out=warm[:], in_=ident[:, 0:1], func=TANH)

        kw_codes = const.tile([P, K_PASSES, H_PASSES, K_PASS], U32, align_bytes=64)
        kw_scales = const.tile([P, K_PASSES, H_PASSES, K_PASS], U8, align_bytes=64)
        bases_codes = const.tile([P, K_PASSES, OI], U32, align_bytes=64)
        bases_scales = const.tile([P, K_PASSES, OI], U8, align_bytes=64)
        base_all = const.tile([P, OI], F32)

        kw_grouped_tiles = {}

        def regroup_kw(G, g, quads, copy_out):
            if (G, g) not in kw_grouped_tiles:
                kw_grouped_tiles[G, g] = setup.tile(
                    [P, K_PASS, PACK], BF16, name="kw_grouped", align_bytes=64, bufs=4
                )
            cols = slice(quads[0] * P, (quads[-1] + 1) * P)
            copy_out(
                out=kw_grouped_tiles[G, g][:, cols, :].rearrange("p (c i) t -> p c t i", i=4),
                in_=kw_raw[:, G, g * PACK : (g + 1) * PACK, cols].rearrange(
                    "p t (c i) -> p c t i", i=4
                ),
            )

        def quantise_kw(G, g):
            nc.vector.quantize_mx(
                out=kw_codes[:, G, g, :].bitcast(FP8X4),
                scales=kw_scales[:, G, g, :],
                in_=kw_grouped_tiles[G, g][:].rearrange("p k t -> p (k t)"),
            )

        def spread_base():
            base_bank = psum_s2.tile([P, BANK], F32, name="s2_bank")
            nc.tensor.matmul(
                base_bank[:, 0:OI], lhsT=ones[:], rhs=base_row[:], start=True, stop=True
            )
            nc.scalar.copy(out=base_all[:], in_=base_bank[:, 0:OI])

        bases_grouped = setup.tile([P, K_PASSES, OI, PACK], BF16, align_bytes=64)

        def regroup_bases():
            for G in range(K_PASSES):
                nc.vector.tensor_copy(
                    out=bases_grouped[:, G, :, :].rearrange("p (c i) t -> p c t i", i=4),
                    in_=bases_raw[:, G * PACK : (G + 1) * PACK, :].rearrange(
                        "p t (c i) -> p c t i", i=4
                    ),
                )

        def quantise_bases():
            nc.vector.quantize_mx(
                out=bases_codes[:].rearrange("p G n -> p (G n)").bitcast(FP8X4),
                scales=bases_scales[:].rearrange("p G n -> p (G n)"),
                in_=bases_grouped[:].rearrange("p G n t -> p (G n t)"),
            )

        def transpose_hk(unit, pair):
            c, g = divmod(unit, H_PASSES)
            hk_words = hk_tiles[c][:].rearrange("p j h -> p (j h)").bitcast(F32)
            words_per_row = H // 2
            if (unit < 2 and unit % 2 == 1) or (unit in (2, 3) and pair == 1):
                hk_bank = psum_co.tile([P, BANK], F32, name="co_bank")
            else:
                hk_bank = psum_hk.tile([P, BANK], F32)
            for u in range(2):
                for jj in range(2):
                    first = (2 * pair + jj) * words_per_row + (2 * g + u) * P
                    nc.tensor.transpose(
                        hk_bank[:, (2 * u + jj) * P : (2 * u + jj + 1) * P],
                        hk_words[:, first : first + P],
                        ident[:],
                    )
            hk_banks[unit, pair] = hk_bank

        def empty_hk(unit, pair, copy_out):
            if unit not in hk_grouped_tiles:
                hk_grouped_tiles[unit] = stream.tile(
                    [P, CHUNK * PACK], BF16, name="hk_grouped", align_bytes=64, bufs=4
                )
            grouped_words = hk_grouped_tiles[unit][:].bitcast(F32).rearrange("p (b u) -> p b u", u=2)
            copy_out(
                out=grouped_words[:, 2 * pair * P : (2 * pair + 2) * P, :],
                in_=hk_banks[unit, pair][:].rearrange("p (u b) -> p b u", u=2),
            )

        def quantise_hk(unit):
            hk_codes = stream.tile([P, CHUNK], U32, align_bytes=64, bufs=7)
            hk_scales = stream.tile([P, CHUNK], U8, align_bytes=64, bufs=7)
            nc.vector.quantize_mx(
                out=hk_codes[:].bitcast(FP8X4),
                scales=hk_scales[:],
                in_=hk_grouped_tiles[unit][:],
            )
            hk_quantised[unit] = (hk_codes, hk_scales)

        def stage_1(s, t, passes=range(H_PASSES)):
            c, G = divmod(s, K_PASSES)
            if passes[0] == 0:
                if s < 2 and t == PACK - 1:
                    s1_banks[s, t] = psum_s2.tile([P, BANK], F32, name="s2_bank")
                else:
                    s1_banks[s, t] = psum_s1.tile([P, BANK], F32, name="s1_bank")
            for g in passes:
                hk_codes, hk_scales = hk_quantised[c * H_PASSES + g]
                nc.tensor.matmul_mx(
                    out=s1_banks[s, t][:],
                    lhsT=kw_codes[:, G, g, t * P : (t + 1) * P].bitcast(FP8X4),
                    lhsT_scale=kw_scales[:, G, g, t * P : (t + 1) * P],
                    rhs=hk_codes[:].bitcast(FP8X4),
                    rhs_scale=hk_scales[:],
                    start=(g == 0),
                    stop=(g == H_PASSES - 1),
                )

        def tanh(s, t):
            if t == 0:
                coeff_t_tiles[s] = stream.tile([P, PACK, CHUNK], F32, name="coeff_t", bufs=4)
            m = s % K_PASSES * PACK + t
            nc.scalar.activation(
                out=coeff_t_tiles[s][:, t, :],
                in_=s1_banks[s, t][:],
                func=TANH,
                bias=kb[:, m : m + 1],
            )

        def regroup_coeff(s, tiles=range(CHUNK_TILES)):
            if tiles[0] == 0:
                coeff_grouped_tiles[s] = stream.tile(
                    [P, CHUNK, PACK], BF16, name="coeff_grouped", align_bytes=64
                )
            a, b = tiles[0], tiles[-1] + 1
            grouped = coeff_grouped_tiles[s][:, a * P : b * P, :]
            nc.vector.tensor_copy(
                out=grouped.rearrange("p (c i) t -> p c t i", i=4),
                in_=coeff_t_tiles[s][:, :, a * P : b * P].rearrange("p t (c i) -> p c t i", i=4),
            )

        def quantise_coeff(s, tiles=range(CHUNK_TILES)):
            if tiles[0] == 0:
                coeff_codes = stream.tile([P, CHUNK], U32, align_bytes=64, bufs=8)
                coeff_scales = stream.tile([P, CHUNK], U8, align_bytes=64, bufs=8)
                coeff_quantised[s] = (coeff_codes, coeff_scales)
            coeff_codes, coeff_scales = coeff_quantised[s]
            cols = slice(tiles[0] * P, (tiles[-1] + 1) * P)
            nc.vector.quantize_mx(
                out=coeff_codes[:, cols].bitcast(FP8X4),
                scales=coeff_scales[:, cols],
                in_=coeff_grouped_tiles[s][:, cols, :].rearrange("p b t -> p (b t)"),
            )

        def transpose_coeff(s, j):
            if s == STEPS - 1 and j < 2:
                co_bank = psum_s1.tile([P, BANK], F32, name="s1_bank")
            elif s == STEPS - 2 and j >= 2:
                co_bank = psum_hk.tile([P, BANK], F32, name="hk_bank")
            else:
                co_bank = psum_co.tile([P, BANK], F32)
            for t in range(PACK):
                nc.tensor.transpose(
                    co_bank[:, t * P : (t + 1) * P],
                    coeff_t_tiles[s][:, t, j * P : (j + 1) * P],
                    ident[:],
                )
            co_banks[s, j] = co_bank

        def empty_coeff(s, j, copy_out):
            c, G = divmod(s, K_PASSES)
            if j % 2 == 0:
                coeff_sb_tiles[s, j // 2] = stream.tile([P, 2, BANK], F32, name="coeff_sb", bufs=4)
            coeff_sb = coeff_sb_tiles[s, j // 2]
            copy_out(out=coeff_sb[:, j % 2, :], in_=co_banks[s, j][:])
            if s >= STEPS - 2:
                nc.sync.dma_start(
                    out=coeff_rows[c, :, j, G * BANK : (G + 1) * BANK], in_=coeff_sb[:, j % 2, :]
                )
            elif j % 2 == 1:
                nc.sync.dma_start(
                    out=coeff_rows[c, :, j - 1 : j + 1, G * BANK : (G + 1) * BANK], in_=coeff_sb[:]
                )

        def compute_gains(v, multiply):
            c, pair = divmod(v, 2)
            tiles = slice(2 * pair, 2 * pair + 2)
            gains = stream.tile([P, 2, O, I], F32, bufs=GAINS_BUFS)
            multiply_gains(
                multiply, gains, row_sb[:, c, tiles, :], col_sb[:, c, tiles, :]
            )
            gains_tiles[v] = gains

        def stage_2(v):
            c, pair = divmod(v, 2)
            if v == PAIRS - 1 or v % 2 == 1 and PAIRS - 6 < v:
                s2_bank = psum_s1.tile([P, 2, OI], F32, name="s1_bank")
            else:
                s2_bank = psum_s2.tile([P, 2, OI], F32)
            for jj in range(2):
                j = 2 * pair + jj
                for G in range(K_PASSES):
                    coeff_codes, coeff_scales = coeff_quantised[c * K_PASSES + G]
                    nc.tensor.matmul_mx(
                        out=s2_bank[:, jj, :],
                        lhsT=coeff_codes[:, j * P : (j + 1) * P].bitcast(FP8X4),
                        lhsT_scale=coeff_scales[:, j * P : (j + 1) * P],
                        rhs=bases_codes[:, G, :].bitcast(FP8X4),
                        rhs_scale=bases_scales[:, G, :],
                        start=(G == 0),
                        stop=(G == K_PASSES - 1),
                    )
            s2_banks[v] = s2_bank

        def add_base(v):
            summed = stream.tile([P, 2, OI], F32, bufs=3)
            nc.vector.tensor_tensor(
                out=summed[:],
                in0=s2_banks[v][:],
                in1=base_all[:].unsqueeze(1).to_broadcast([P, 2, OI]),
                op=ADD,
            )
            summed_tiles[v] = summed

        def scale_weight(v):
            c, pair = divmod(v, 2)
            weight_sb = stream.tile([P, 2, OI], F32, bufs=3)
            nc.vector.tensor_tensor(
                out=weight_sb[:],
                in0=summed_tiles[v][:],
                in1=gains_tiles[v][:].rearrange("p j o i -> p j (o i)"),
                op=MULT,
            )
            nc.sync.dma_start(out=weight_rows[c, :, 2 * pair : 2 * pair + 2, :], in_=weight_sb[:])
            if v + GAINS_BUFS < PAIRS:
                compute_gains(v + GAINS_BUFS, nc.gpsimd.tensor_tensor)

        GS = 4
        CO_LAG = 3
        BOTH = range(5, HK_UNITS - 4)
        LOW = range(0, 2)
        HIGH = range(2, 4)
        ALL = range(4)
        copy_v = nc.vector.tensor_copy
        copy_s = nc.scalar.copy

        def co_half(k, copies=None):
            if 0 <= k < 2 * STEPS:
                for i, j in enumerate((2 * (k % 2), 2 * (k % 2) + 1)):
                    transpose_coeff(k // 2, j)
                    empty_coeff(k // 2, j, copies[i] if copies else copy_s)

        MIDDLE = {STEPS - 2: STEPS - 5, STEPS - 1: STEPS - 3}
        END = {s: s - STAGE_2_LAG for s in range(STAGE_2_LAG, STEPS - 2)}
        END[STEPS - 2] = STEPS - 4

        def step(s):
            before = END.get(s - 1)
            middle = MIDDLE.get(s)
            unit = s + 3
            if s % 2 == 0 and s // 2 + 4 < CHUNKS:
                load_hk(s // 2 + 4)
            if before:
                scale_weight(before - 1)
            if 3 < s and unit - 1 < HK_UNITS:
                empty_hk(unit - 1, 0, copy_v)
                if s - 1 in BOTH:
                    empty_hk(unit - 1, 1, copy_v)
            if before is not None:
                add_base(before)
            for r in range(2):
                for t in (2 * r, 2 * r + 1):
                    stage_1(s, t)
                    tanh(s, t)
                if s == 2 and r == 1:
                    keep_clock(1)
                if r == 0 and middle is not None:
                    stage_2(middle)
                if r == 1 and s in END:
                    stage_2(END[s])
                co_half(2 * s + r - CO_LAG)
                if s == 2:
                    for pair in range(2):
                        transpose_hk(4 + r, pair)
                        empty_hk(4 + r, pair, (copy_v, copy_s)[r])
                    quantise_hk(4 + r)
                elif unit < HK_UNITS:
                    transpose_hk(unit, r)
                    if r == 1 and s not in BOTH:
                        empty_hk(unit, r, copy_s)
                if r == 0:
                    regroup_coeff(s - 1)
                    if 3 < s and unit - 1 < HK_UNITS:
                        quantise_hk(unit - 1)
                    if middle is not None:
                        scale_weight(middle - 1)
                    quantise_coeff(s - 1)
                    for w in range(2 * s - 2 * GS, 2 * s - 2 * GS + 2):
                        if 0 <= w < GAINS_BUFS:
                            compute_gains(w, nc.vector.tensor_tensor)
                    if middle is not None:
                        add_base(middle)
                if s == 2 and r == 0:
                    regroup_bases()
                    quantise_bases()

        def start():
            regroup_kw(0, 0, ALL, copy_v)
            quantise_kw(0, 0)
            for pair in range(2):
                for unit in range(2):
                    transpose_hk(unit, pair)
                    empty_hk(unit, pair, copy_s)
            keep_clock(3)
            regroup_kw(0, 1, range(0, 3), copy_v)
            regroup_kw(0, 1, range(3, 4), copy_s)
            prepare_bias()
            spread_base()
            quantise_hk(0)
            quantise_hk(1)
            quantise_kw(0, 1)
            for t in range(4):
                stage_1(0, t, (0,))
            regroup_kw(1, 1, HIGH, copy_s)
            regroup_kw(1, 0, ALL, copy_v)
            regroup_kw(1, 1, LOW, copy_v)
            for t in range(4):
                stage_1(0, t, (1,))
                tanh(0, t)
            quantise_kw(1, 0)
            quantise_kw(1, 1)
            for pair in range(2):
                for unit in (2, 3):
                    transpose_hk(unit, pair)
                    empty_hk(unit, pair, (copy_s, copy_v)[pair])
            for t in range(4):
                stage_1(1, t)
                tanh(1, t)
            quantise_hk(2)
            quantise_hk(3)
            co_half(0, (copy_v, copy_v))
            regroup_coeff(0)
            quantise_coeff(0)
            load_hk(4)

        def tail():
            last = STEPS - 1
            v = STEPS - 2
            co_half(2 * last - 1)
            regroup_coeff(last, LOW)
            regroup_coeff(last, HIGH)
            quantise_coeff(last, LOW)
            quantise_coeff(last, HIGH)
            scale_weight(v - 1)
            keep_clock(3)
            co_half(2 * last, (copy_s, copy_v))
            stage_2(v)
            co_half(2 * last + 1)
            stage_2(v + 1)
            add_base(v)
            scale_weight(v)
            add_base(v + 1)
            scale_weight(v + 1)

        start()
        for s in range(2, STEPS):
            step(s)
        tail()
